import numpy as np
import ml_dtypes


def mxq(x, axis, fmt="e4m3"):
    dtype, down = {"e4m3": (ml_dtypes.float8_e4m3fn, 7), "e5m2": (ml_dtypes.float8_e5m2, 14)}[fmt]
    v = np.moveaxis(np.asarray(x, np.float32).astype(ml_dtypes.bfloat16).astype(np.float64), axis, -1)
    blocks = v.reshape(v.shape[:-1] + (-1, 32))
    amax = np.abs(blocks).max(-1, keepdims=True)
    byte = np.maximum(np.where(amax > 0, np.frexp(amax)[1] - 1 + 127, 0) - down, 1)
    scale = np.exp2(byte - 127.0)
    codes = (blocks / scale).astype(np.float32).astype(dtype).astype(np.float64)
    return np.moveaxis((codes * scale).reshape(v.shape), -1, axis)


WIDE = False


def mx_kscale(k):
    if not WIDE:
        return np.ones(k)
    levels = np.array([10, -10, 5, -5, 0])
    a = np.random.permutation(np.resize(levels, k // 512 * 4)).reshape(k // 512, 4)
    idx = np.arange(k)
    return np.exp2(a[idx // 512, idx % 128 // 32])


BF16 = ml_dtypes.bfloat16


def bf(x):
    return np.asarray(x, np.float32).astype(BF16)


def f64(x):
    return np.asarray(x).astype(np.float64)


B, D, HH, WW, P, R = 4, 512, 32, 32, 256, 16

EPSILON = 1e-05
C = 1.0


def expmap0(u, c):
    sc = np.sqrt(c)
    norm = np.maximum(np.sqrt(np.sum(u * u, axis=-1, keepdims=True)), 1e-15)
    return np.tanh(sc * norm) * u / (sc * norm)


def asinh(v):
    a = np.abs(v)
    return np.sign(v) * np.where(a < 0.01, a - a ** 3 / 6.0, np.log(a + np.sqrt(a * a + 1.0)))


def draw(n, a, b, basis):
    return a * (np.random.standard_normal((n, R)) @ basis) / np.sqrt(R) + b * np.random.standard_normal((n, D)) / np.sqrt(D)


def setup_inputs():
    basis = np.random.standard_normal((R, D)) / np.sqrt(D)
    s = mx_kscale(D)
    sn = s / 2.0 ** np.round(0.5 * np.log2(np.mean(s * s)))
    z = np.moveaxis((draw(B * HH * WW, 0.8, 0.5, basis) * sn).reshape(B, HH, WW, D), -1, 1)
    p = expmap0(draw(P, 0.55, 0.3, basis) * sn, C)
    dirs = draw(P, 1.0, 0.4, basis)
    normals = dirs / np.sqrt(np.sum(dirs * dirs, axis=-1, keepdims=True)) * (1.0 + 0.1 * np.random.standard_normal((P, 1))) / sn
    return {"z": bf(np.ascontiguousarray(z)), "p": bf(p), "normals": bf(normals)}


def reference(z, p, normals):
    z, p, normals = f64(z), f64(p), f64(normals)
    c = C
    c_sqrt = np.sqrt(c)

    z = np.ascontiguousarray(np.moveaxis(expmap0(np.moveaxis(z, 1, -1), c), -1, 1))

    p_hat = -p
    zq = mxq(z, 1, "e4m3").reshape(B, D, HH * WW)
    p_dot_z = (mxq(p_hat, 1, "e4m3") @ zq).reshape(B, P, HH, WW)
    z_dot_w = (mxq(normals, 1, "e4m3") @ zq).reshape(B, P, HH, WW)

    z_norm = np.sum(z * z, axis=1, keepdims=True)
    p_norm = np.sum(p * p, axis=-1)[None, :, None, None]
    w_norm = np.sum(normals * normals, axis=-1)[None, :, None, None]
    p_dot_w = np.sum(p_hat * normals, axis=-1)[None, :, None, None]

    lambda_p_c = 2.0
    denom = np.maximum(1 + 2 * c * p_dot_z + c ** 2 * z_norm * p_norm, EPSILON)
    alpha = (1 + 2 * c * p_dot_z + c * z_norm) / denom
    beta = (1 - c * p_norm) / denom

    p_m_y_w = alpha * p_dot_w + beta * z_dot_w
    p_m_y_w_norm = alpha ** 2 * p_norm + 2 * alpha * beta * p_dot_z + beta ** 2 * z_norm

    arg = np.minimum(
        2 * c_sqrt * p_m_y_w / np.maximum((1 - c * p_m_y_w_norm) * w_norm, EPSILON),
        85.0,
    )
    logits = lambda_p_c * w_norm / c_sqrt * asinh(arg)
    return -logits

@@ -1,0 +1,371 @@
+import math
+from contextlib import ExitStack
+
+import concourse.mybir as mybir
+from concourse.masks import make_identity
+
+F32 = mybir.dt.float32
+BF16 = mybir.dt.bfloat16
+U32 = mybir.dt.uint32
+U8 = mybir.dt.uint8
+FP8X4 = mybir.dt.float8_e4m3fn_x4
+ALU = mybir.AluOpType
+ACT = mybir.ActivationFunctionType
+AX = mybir.AxisListType
+
+P = 128
+NB = 4
+NPX = 1024
+BLK = 512
+CT = 2
+D = 512
+FLOPS = 2 * 2 * 256 * D * NB * NPX
+
+A85 = math.log(85.0 + math.sqrt(85.0 * 85.0 + 1.0))
+THR6 = 0.01 * 0.01 / 6.0
+
+
+def tile_hyperboliclayer_kernel(tc, z, p, normals, out):
+    nc = tc.nc
+    with ExitStack() as ctx:
+        ctx.enter_context(tc.manual_schedule())
+        keep = ctx.enter_context(tc.tile_pool(name="keep", bufs=1))
+        psum = ctx.enter_context(tc.psum_pool(name="psum", bufs=2))
+
+        ident_b = keep.tile([P, P], BF16, name="ident_b")
+        make_identity(nc, ident_b[:])
+        ident_f = keep.tile([P, P], F32, name="ident_f")
+        make_identity(nc, ident_f[:])
+        ones2 = keep.tile([P, 2], F32, name="ones2")
+        nc.vector.memset(ones2[:], 1.0)
+
+        p_raw = keep.tile([P, CT, D], BF16, name="p_raw")
+        n_raw = keep.tile([P, CT, D], BF16, name="n_raw")
+        nc.scalar.dma_start(out=p_raw[:], in_=p.rearrange("(c k) d -> k c d", k=P))
+        nc.scalar.dma_start(out=n_raw[:], in_=normals.rearrange("(c k) d -> k c d", k=P))
+        zt = []
+        for b in range(NB):
+            zb = keep.tile([P, 4, NPX], BF16, name="z%d" % b)
+            nc.sync.dma_start(out=zb[:], in_=z[b].rearrange("(q j) h w -> q j (h w)", j=4))
+            zt.append(zb)
+
+        warm = keep.tile([P, 1], F32, name="warm")
+        nc.scalar.activation(out=warm[:], in_=ones2[:, 0:1], func=ACT.Sqrt)
+
+        w_codes = keep.tile([P, 4 * P], U32, name="w_codes", align_bytes=64)
+        w_scales = keep.tile([P, 4 * P], U8, name="w_scales", align_bytes=64)
+        ppww = keep.tile([P, 4], F32, name="ppww")
+        pwp = keep.tile([P, CT], F32, name="pwp")
+
+        def col(name):
+            return keep.tile([P, CT], F32, name=name)
+
+        bc = col("bc")
+        rb = col("rb")
+        rr = col("rr")
+        nb = col("nb")
+        b2 = col("b2")
+        bw = col("bw")
+        ke = col("ke")
+        bw5 = col("bw5")
+        lnk = col("lnk")
+        rw = col("rw")
+        c2 = col("c2")
+        c2s = col("c2s")
+        w2 = col("w2")
+        cap = col("cap")
+        s_c = keep.tile([P, 32], F32, name="s_c")
+        uh_c = keep.tile([P, 32], F32, name="uh_c")
+        rv_c = keep.tile([P, 32], F32, name="rv_c")
+        uh_t = keep.tile([P, NB * NPX], F32, name="uh_t")
+        rv_t = keep.tile([P, NB * NPX], F32, name="rv_t")
+
+        with tc.tile_pool(name="head", bufs=1) as head:
+            wg = head.tile([P, 4, P, 4], BF16, name="wg", align_bytes=64)
+            for i in range(4):
+                raw = p_raw if i < 2 else n_raw
+                src = raw[:, i % 2, :].rearrange("k (q t) -> k t q", t=4)
+                mg = head.tile([P, 4, P], BF16, name="mg%d" % i)
+                if i < 2:
+                    nc.vector.tensor_scalar(out=mg[:], in0=src, scalar1=-1.0, scalar2=None, op0=ALU.mult)
+                else:
+                    nc.vector.tensor_copy(out=mg[:], in_=src)
+                tp = psum.tile([P, 4, P], BF16, tag="st", name="tp%d" % i)
+                for t in range(4):
+                    nc.tensor.transpose(out=tp[:, t, :], in_=mg[:, t, :], identity=ident_b[:])
+                nc.vector.tensor_copy(out=wg[:, i, :, :], in_=tp[:].rearrange("q t k -> q k t"))
+            nc.vector.quantize_mx(
+                out=w_codes[:].bitcast(FP8X4),
+                scales=w_scales[:],
+                in_=wg[:].rearrange("q i k t -> q (i k t)"),
+            )
+            junk = head.tile([P, D], F32, name="junk")
+            for c in range(CT):
+                nc.scalar.activation(out=junk[:], in_=p_raw[:, c, :], func=ACT.Square, accum_out=ppww[:, c : c + 1])
+            for c in range(CT):
+                nc.scalar.activation(
+                    out=junk[:], in_=n_raw[:, c, :], func=ACT.Square, accum_out=ppww[:, 2 + c : 3 + c]
+                )
+            pn = head.tile([P, CT, D], F32, name="pn")
+            nc.vector.tensor_tensor(out=pn[:], in0=p_raw[:], in1=n_raw[:], op=ALU.mult)
+            nc.vector.reduce_sum(out=pwp[:], in_=pn[:], axis=AX.X)
+            pp = ppww[:, 0:2]
+            ww = ppww[:, 2:4]
+            nc.vector.tensor_scalar(out=bc[:], in0=pp, scalar1=-1.0, scalar2=1.0, op0=ALU.mult, op1=ALU.add)
+            nc.vector.reciprocal(out=rb[:], in_=bc[:])
+            nc.vector.scalar_tensor_tensor(out=rr[:], in0=pwp[:], scalar=-2.0, in1=rb[:], op0=ALU.mult, op1=ALU.mult)
+            nc.vector.tensor_scalar(out=nb[:], in0=bc[:], scalar1=-1.0, scalar2=None, op0=ALU.mult)
+            nc.vector.tensor_scalar(out=b2[:], in0=bc[:], scalar1=0.5, scalar2=None, op0=ALU.mult)
+            nc.vector.tensor_tensor(out=bw[:], in0=bc[:], in1=ww, op=ALU.mult)
+            nc.vector.tensor_scalar(out=ke[:], in0=bw[:], scalar1=1.0e10, scalar2=None, op0=ALU.mult)
+            nc.vector.tensor_scalar(out=bw5[:], in0=bw[:], scalar1=0.5e5, scalar2=None, op0=ALU.mult)
+            nc.vector.reciprocal(out=rw[:], in_=ww)
+            nc.vector.tensor_scalar(out=c2[:], in0=rw[:], scalar1=2.0, scalar2=None, op0=ALU.mult)
+            nc.vector.tensor_scalar(out=c2s[:], in0=rw[:], scalar1=2.0 / math.sqrt(6.0), scalar2=None, op0=ALU.mult)
+            nc.vector.tensor_scalar(out=w2[:], in0=ww, scalar1=2.0, scalar2=None, op0=ALU.mult)
+            nc.vector.tensor_scalar(out=cap[:], in0=ww, scalar1=-2.0 * A85, scalar2=None, op0=ALU.mult)
+
+            nsq_c = head.tile([P, 32], F32, name="nsq_c")
+            nts = []
+            for b in range(NB):
+                sq_s = head.tile([P, 2, NPX], F32, name="sqs%d" % b)
+                sq_v = head.tile([P, 2, NPX], F32, name="sqv%d" % b)
+                nc.scalar.activation(out=sq_s[:], in_=zt[b][:, 0:2, :], func=ACT.Square)
+                nc.vector.tensor_tensor(out=sq_v[:], in0=zt[b][:, 2:4, :], in1=zt[b][:, 2:4, :], op=ALU.mult)
+                for hb in range(2):
+                    nt = psum.tile([P, 4, P], F32, tag=("a", "w", "sb", "st")[b], name="nt")
+                    for c4 in range(4):
+                        c8 = hb * 4 + c4
+                        for j in range(4):
+                            sq = sq_s if j < 2 else sq_v
+                            nc.tensor.matmul(
+                                out=nt[:, c4, :],
+                                lhsT=sq[:, j % 2, c8 * P : (c8 + 1) * P],
+                                rhs=ident_f[:],
+                                is_transpose=True,
+                                start=(j == 0),
+                                stop=(j == 3),
+                            )
+                    nts.append(nt)
+            for k in range(2 * NB):
+                nc.vector.reduce_sum(out=nsq_c[:, 4 * k : 4 * k + 4], in_=nts[k][:], axis=AX.X)
+            nrm = head.tile([P, 32], F32, name="nrm")
+            th = head.tile([P, 32], F32, name="th")
+            rn = head.tile([P, 32], F32, name="rn")
+            zz = head.tile([P, 32], F32, name="zz")
+            vv = head.tile([P, 32], F32, name="vv")
+            nc.vector.tensor_scalar(out=nrm[:], in0=nsq_c[:], scalar1=1.0e-30, scalar2=None, op0=ALU.max)
+            nc.scalar.activation(out=nrm[:], in_=nrm[:], func=ACT.Sqrt)
+            nc.scalar.activation(out=th[:], in_=nrm[:], func=ACT.Tanh)
+            nc.vector.reciprocal(out=rn[:], in_=nrm[:])
+            nc.vector.tensor_tensor(out=s_c[:], in0=th[:], in1=rn[:], op=ALU.mult)
+            nc.vector.tensor_tensor(out=zz[:], in0=th[:], in1=th[:], op=ALU.mult)
+            nc.vector.tensor_scalar(out=uh_c[:], in0=zz[:], scalar1=0.5, scalar2=0.5, op0=ALU.mult, op1=ALU.add)
+            nc.vector.tensor_scalar(out=vv[:], in0=zz[:], scalar1=-1.0, scalar2=1.0, op0=ALU.mult, op1=ALU.add)
+            nc.vector.reciprocal(out=rv_c[:], in_=vv[:])
+
+        ep = ctx.enter_context(tc.tile_pool(name="ep", bufs=2))
+        st = {}
+
+        def bcast(dst, comp, blk):
+            for i in range(4):
+                cc = blk * 4 + i
+                nc.tensor.transpose(
+                    out=dst[:, i * P : (i + 1) * P],
+                    in_=comp[:, cc : cc + 1].to_broadcast([P, P]),
+                    identity=ident_f[:],
+                )
+
+        def stage_ev(i):
+            for comp, dst in ((uh_c, uh_t), (rv_c, rv_t)):
+                for h in range(2):
+                    blk = 2 * i + h
+                    stg = psum.tile([P, BLK], F32, tag="st", name="stg")
+                    bcast(stg, comp, blk)
+                    nc.scalar.copy(out=dst[:, blk * BLK : (blk + 1) * BLK], in_=stg[:])
+
+        def stage_y(i):
+            yg = ep.tile([P, NPX, 4], BF16, tag="yg", name="yg", align_bytes=64)
+            for h in range(2):
+                sb = psum.tile([P, BLK], F32, tag="sb", name="sb")
+                bcast(sb, s_c, 2 * i + h)
+                nc.vector.tensor_tensor(
+                    out=yg[:, h * BLK : (h + 1) * BLK, :],
+                    in0=zt[i][:, :, h * BLK : (h + 1) * BLK].rearrange("q j n -> q n j"),
+                    in1=sb[:].unsqueeze(2).to_broadcast([P, BLK, 4]),
+                    op=ALU.mult,
+                )
+            yc = ep.tile([P, NPX], U32, tag="yc", name="yc", align_bytes=64)
+            ys = ep.tile([P, NPX], U8, tag="ys", name="ys", align_bytes=64)
+            nc.vector.quantize_mx(out=yc[:].bitcast(FP8X4), scales=ys[:], in_=yg[:].rearrange("q n j -> q (n j)"))
+            st[("yc", i)] = yc
+            st[("ys", i)] = ys
+
+        def mx(dst, op_i, i, h):
+            yc = st[("yc", i)]
+            ys = st[("ys", i)]
+            nc.tensor.matmul_mx(
+                out=dst[:],
+                lhsT=w_codes[:, op_i * P : (op_i + 1) * P].bitcast(FP8X4),
+                lhsT_scale=w_scales[:, op_i * P : (op_i + 1) * P],
+                rhs=yc[:, h * BLK : (h + 1) * BLK].bitcast(FP8X4),
+                rhs_scale=ys[:, h * BLK : (h + 1) * BLK],
+                start=True,
+                stop=True,
+            )
+
+        def stage_a(i):
+            for c in range(CT):
+                e1 = ep.tile([P, NPX], F32, tag="e1", name="e1")
+                gp = ep.tile([P, NPX], F32, tag="gp", name="gp", bufs=4)
+                dd = ep.tile([P, NPX], F32, tag="dd", name="dd")
+                aps = []
+                wps = []
+                for h in range(2):
+                    a_ps = psum.tile([P, BLK], F32, tag="a", name="a_ps")
+                    w_ps = psum.tile([P, BLK], F32, tag="w", name="w_ps")
+                    mx(a_ps, c, i, h)
+                    mx(w_ps, 2 + c, i, h)
+                    aps.append(a_ps)
+                    wps.append(w_ps)
+                for h in range(2):
+                    nc.vector.tensor_tensor(
+                        out=e1[:, h * BLK : (h + 1) * BLK],
+                        in0=aps[h][:],
+                        in1=uh_t[:, i * NPX + h * BLK : i * NPX + (h + 1) * BLK],
+                        op=ALU.add,
+                    )
+                for h in range(2):
+                    nc.vector.scalar_tensor_tensor(
+                        out=gp[:, h * BLK : (h + 1) * BLK],
+                        in0=e1[:, h * BLK : (h + 1) * BLK],
+                        scalar=rr[:, c : c + 1],
+                        in1=wps[h][:],
+                        op0=ALU.mult,
+                        op1=ALU.add,
+                    )
+                nc.vector.scalar_tensor_tensor(
+                    out=dd[:],
+                    in0=uh_t[:, i * NPX : (i + 1) * NPX],
+                    scalar=nb[:, c : c + 1],
+                    in1=e1[:],
+                    op0=ALU.mult,
+                    op1=ALU.add,
+                )
+                st[("gp", i, c)] = gp
+                st[("dd", i, c)] = dd
+
+        def stage_sa(i):
+            for c in range(CT):
+                dd = st[("dd", i, c)]
+                nc.scalar.activation(out=dd[:], in_=dd[:], func=ACT.Ln, bias=b2[:, c : c + 1], scale=1.0)
+
+        def stage_sb(i):
+            for c in range(CT):
+                dd = st[("dd", i, c)]
+                nc.scalar.activation(out=dd[:], in_=dd[:], func=ACT.Exp, bias=lnk[:, c : c + 1], scale=-1.0)
+
+        def stage_b(i):
+            for c in range(CT):
+                dd = st[("dd", i, c)]
+                nc.vector.scalar_tensor_tensor(
+                    out=dd[:],
+                    in0=dd[:],
+                    scalar=ke[:, c : c + 1],
+                    in1=rv_t[:, i * NPX : (i + 1) * NPX],
+                    op0=ALU.min,
+                    op1=ALU.min,
+                )
+            for c in range(CT):
+                gp = st[("gp", i, c)]
+                nc.vector.tensor_tensor(out=gp[:], in0=gp[:], in1=st[("dd", i, c)][:], op=ALU.mult)
+
+        def stage_sc(i):
+            for c in range(CT):
+                gp = st[("gp", i, c)]
+                q6 = ep.tile([P, NPX], F32, tag="q6", name="q6")
+                xa = ep.tile([P, NPX], F32, tag="xa", name="xa")
+                sg = ep.tile([P, NPX], F32, tag="sg", name="sg")
+                nc.scalar.activation(out=q6[:], in_=gp[:], func=ACT.Square, scale=c2s[:, c : c + 1])
+                nc.scalar.activation(out=xa[:], in_=gp[:], func=ACT.Abs, scale=c2[:, c : c + 1])
+                nc.scalar.activation(out=sg[:], in_=gp[:], func=ACT.Sign)
+                st[("q6", i, c)] = q6
+                st[("xa", i, c)] = xa
+                st[("sg", i, c)] = sg
+            for c in range(CT):
+                lt = ep.tile([P, NPX], F32, tag="lt", name="lt")
+                nc.scalar.activation(out=lt[:], in_=st[("q6", i, c)][:], func=ACT.Sqrt, bias=ones2[:, 0:1], scale=6.0)
+                st[("lt", i, c)] = lt
+
+        def stage_c(i):
+            for c in range(CT):
+                lt = st[("lt", i, c)]
+                nc.vector.tensor_tensor(out=lt[:], in0=lt[:], in1=st[("xa", i, c)][:], op=ALU.add)
+            for c in range(CT):
+                ns = ep.tile([P, NPX], F32, tag="ns", name="ns")
+                nc.vector.scalar_tensor_tensor(
+                    out=ns[:],
+                    in0=st[("q6", i, c)][:],
+                    scalar=1.0,
+                    in1=st[("xa", i, c)][:],
+                    op0=ALU.subtract,
+                    op1=ALU.mult,
+                )
+                st[("ns", i, c)] = ns
+
+        def stage_sd(i):
+            for c in range(CT):
+                lt = st[("lt", i, c)]
+                nc.scalar.activation(out=lt[:], in_=lt[:], func=ACT.Ln)
+
+        def stage_d(i):
+            for c in range(CT):
+                lt = st[("lt", i, c)]
+                nc.vector.scalar_tensor_tensor(
+                    out=lt[:], in0=st[("q6", i, c)][:], scalar=THR6, in1=lt[:], op0=ALU.is_ge, op1=ALU.mult
+                )
+            for c in range(CT):
+                lt = st[("lt", i, c)]
+                nc.vector.scalar_tensor_tensor(
+                    out=lt[:], in0=lt[:], scalar=-1.0, in1=st[("ns", i, c)][:], op0=ALU.mult, op1=ALU.min
+                )
+            ots = []
+            for c in range(CT):
+                ot = ep.tile([P, NPX], F32, tag="ot", name="ot", bufs=4)
+                nc.vector.scalar_tensor_tensor(
+                    out=ot[:],
+                    in0=st[("lt", i, c)][:],
+                    scalar=w2[:, c : c + 1],
+                    in1=st[("sg", i, c)][:],
+                    op0=ALU.mult,
+                    op1=ALU.mult,
+                )
+                ots.append(ot)
+            for c in range(CT):
+                ot = ots[c]
+                nc.vector.tensor_scalar(out=ot[:], in0=ot[:], scalar1=cap[:, c : c + 1], scalar2=None, op0=ALU.max)
+                nc.sync.dma_start(out=out[i, c * P : (c + 1) * P].rearrange("k h w -> k (h w)"), in_=ot[:])
+
+        stage_y(0)
+        stage_ev(0)
+        stage_a(0)
+        nc.scalar.activation(out=lnk[:], in_=bw5[:], func=ACT.Ln)
+        stage_y(1)
+        for i in range(NB):
+            if i > 0:
+                stage_sd(i - 1)
+            stage_sa(i)
+            stage_sb(i)
+            if i > 0:
+                stage_d(i - 1)
+            if i + 1 < NB:
+                stage_ev(i + 1)
+            stage_b(i)
+            stage_sc(i)
+            if i + 1 < NB:
+                stage_a(i + 1)
+            if i + 2 < NB:
+                stage_y(i + 2)
+            stage_c(i)
+        stage_sd(NB - 1)
+        stage_d(NB - 1)

@@ -22,7 +22,8 @@ D = 512
 FLOPS = 2 * 2 * 256 * D * NB * NPX
 
 A85 = math.log(85.0 + math.sqrt(85.0 * 85.0 + 1.0))
-THR6 = 0.01 * 0.01 / 6.0
+KAPPA = 30000.0
+NBUF = {"aw": 3, "x": 2, "y": 2, "st": 1}
 
 
 def tile_hyperboliclayer_kernel(tc, z, p, normals, out):
@@ -79,6 +80,9 @@ def tile_hyperboliclayer_kernel(tc, z, p, normals, out):
         rv_c = keep.tile([P, 32], F32, name="rv_c")
         uh_t = keep.tile([P, NB * NPX], F32, name="uh_t")
         rv_t = keep.tile([P, NB * NPX], F32, name="rv_t")
+        s_t = keep.tile([P, NB * NPX], F32, name="s_t")
+        mhalf = keep.tile([P, 1], F32, name="mhalf")
+        nc.vector.memset(mhalf[:], -0.5)
 
         with tc.tile_pool(name="head", bufs=1) as head:
             wg = head.tile([P, 4, P, 4], BF16, name="wg", align_bytes=64)
@@ -90,7 +94,7 @@ def tile_hyperboliclayer_kernel(tc, z, p, normals, out):
                     nc.vector.tensor_scalar(out=mg[:], in0=src, scalar1=-1.0, scalar2=None, op0=ALU.mult)
                 else:
                     nc.vector.tensor_copy(out=mg[:], in_=src)
-                tp = psum.tile([P, 4, P], BF16, tag="st", name="tp%d" % i)
+                tp = psum.tile([P, 4, P], BF16, tag=("x", "y")[i % 2], name="tp%d" % i)
                 for t in range(4):
                     nc.tensor.transpose(out=tp[:, t, :], in_=mg[:, t, :], identity=ident_b[:])
                 nc.vector.tensor_copy(out=wg[:, i, :, :], in_=tp[:].rearrange("q t k -> q k t"))
@@ -133,7 +137,8 @@ def tile_hyperboliclayer_kernel(tc, z, p, normals, out):
                 nc.scalar.activation(out=sq_s[:], in_=zt[b][:, 0:2, :], func=ACT.Square)
                 nc.vector.tensor_tensor(out=sq_v[:], in0=zt[b][:, 2:4, :], in1=zt[b][:, 2:4, :], op=ALU.mult)
                 for hb in range(2):
-                    nt = psum.tile([P, 4, P], F32, tag=("a", "w", "sb", "st")[b], name="nt")
+                    tg = ("aw", "aw", "aw", "x", "x", "y", "y", "st")[2 * b + hb]
+                    nt = psum.tile([P, 4, P], F32, tag=tg, name="nt", bufs=NBUF[tg])
                     for c4 in range(4):
                         c8 = hb * 4 + c4
                         for j in range(4):
@@ -167,107 +172,133 @@ def tile_hyperboliclayer_kernel(tc, z, p, normals, out):
         ep = ctx.enter_context(tc.tile_pool(name="ep", bufs=2))
         st = {}
 
+        def ptile(tg, name):
+            return psum.tile([P, 4, P], F32, tag=tg, name=name, bufs=NBUF[tg])
+
+        def flat(t):
+            return t[:].rearrange("q a b -> q (a b)")
+
         def bcast(dst, comp, blk):
-            for i in range(4):
-                cc = blk * 4 + i
+            for j in range(4):
+                cc = blk * 4 + j
                 nc.tensor.transpose(
-                    out=dst[:, i * P : (i + 1) * P],
-                    in_=comp[:, cc : cc + 1].to_broadcast([P, P]),
-                    identity=ident_f[:],
+                    out=dst[:, j, :], in_=comp[:, cc : cc + 1].to_broadcast([P, P]), identity=ident_f[:]
                 )
 
-        def stage_ev(i):
-            for comp, dst in ((uh_c, uh_t), (rv_c, rv_t)):
-                for h in range(2):
-                    blk = 2 * i + h
-                    stg = psum.tile([P, BLK], F32, tag="st", name="stg")
-                    bcast(stg, comp, blk)
-                    nc.scalar.copy(out=dst[:, blk * BLK : (blk + 1) * BLK], in_=stg[:])
+        def stage_fill(comp, blk):
+            stg = ptile("st", "stg")
+            bcast(stg, comp, blk)
+            st["stg"] = stg
+
+        def stage_evac(dst, blk):
+            nc.scalar.copy(out=dst[:, blk * BLK : (blk + 1) * BLK], in_=flat(st["stg"]))
+
+        def y_mult(i, h, s_ap):
+            nc.vector.tensor_tensor(
+                out=st[("yg", i)][:, h * BLK : (h + 1) * BLK, :],
+                in0=zt[i][:, :, h * BLK : (h + 1) * BLK].rearrange("q j n -> q n j"),
+                in1=s_ap.unsqueeze(2).to_broadcast([P, BLK, 4]),
+                op=ALU.mult,
+            )
 
         def stage_y(i):
-            yg = ep.tile([P, NPX, 4], BF16, tag="yg", name="yg", align_bytes=64)
+            st[("yg", i)] = ep.tile([P, NPX, 4], BF16, tag="yg", name="yg", align_bytes=64, bufs=1)
             for h in range(2):
-                sb = psum.tile([P, BLK], F32, tag="sb", name="sb")
-                bcast(sb, s_c, 2 * i + h)
-                nc.vector.tensor_tensor(
-                    out=yg[:, h * BLK : (h + 1) * BLK, :],
-                    in0=zt[i][:, :, h * BLK : (h + 1) * BLK].rearrange("q j n -> q n j"),
-                    in1=sb[:].unsqueeze(2).to_broadcast([P, BLK, 4]),
-                    op=ALU.mult,
-                )
+                if i == 0:
+                    sb = ptile("x", "sb")
+                    bcast(sb, s_c, h)
+                    y_mult(i, h, flat(sb))
+                else:
+                    y_mult(i, h, s_t[:, i * NPX + h * BLK : i * NPX + (h + 1) * BLK])
             yc = ep.tile([P, NPX], U32, tag="yc", name="yc", align_bytes=64)
             ys = ep.tile([P, NPX], U8, tag="ys", name="ys", align_bytes=64)
-            nc.vector.quantize_mx(out=yc[:].bitcast(FP8X4), scales=ys[:], in_=yg[:].rearrange("q n j -> q (n j)"))
+            nc.vector.quantize_mx(
+                out=yc[:].bitcast(FP8X4), scales=ys[:], in_=st[("yg", i)][:].rearrange("q n j -> q (n j)")
+            )
             st[("yc", i)] = yc
             st[("ys", i)] = ys
 
-        def mx(dst, op_i, i, h):
-            yc = st[("yc", i)]
-            ys = st[("ys", i)]
+        def mx(op_i, i, h):
+            dst = ptile("aw", "mxo")
             nc.tensor.matmul_mx(
-                out=dst[:],
+                out=flat(dst),
                 lhsT=w_codes[:, op_i * P : (op_i + 1) * P].bitcast(FP8X4),
                 lhsT_scale=w_scales[:, op_i * P : (op_i + 1) * P],
-                rhs=yc[:, h * BLK : (h + 1) * BLK].bitcast(FP8X4),
-                rhs_scale=ys[:, h * BLK : (h + 1) * BLK],
+                rhs=st[("yc", i)][:, h * BLK : (h + 1) * BLK].bitcast(FP8X4),
+                rhs_scale=st[("ys", i)][:, h * BLK : (h + 1) * BLK],
                 start=True,
                 stop=True,
             )
+            st[("mx", i, op_i, h)] = dst
+
+        def hs(h):
+            return slice(h * BLK, (h + 1) * BLK)
+
+        def v1(i, c, h):
+            nc.vector.tensor_tensor(
+                out=st[("e1", i, c)][:, hs(h)],
+                in0=flat(st[("mx", i, c, h)]),
+                in1=uh_t[:, i * NPX + h * BLK : i * NPX + (h + 1) * BLK],
+                op=ALU.add,
+            )
+
+        def v2(i, c, h):
+            nc.vector.scalar_tensor_tensor(
+                out=st[("gp", i, c)][:, hs(h)],
+                in0=st[("e1", i, c)][:, hs(h)],
+                scalar=rr[:, c : c + 1],
+                in1=flat(st[("mx", i, 2 + c, h)]),
+                op0=ALU.mult,
+                op1=ALU.add,
+            )
+
+        def v3(i, c):
+            nc.vector.scalar_tensor_tensor(
+                out=st[("dd", i, c)][:],
+                in0=uh_t[:, i * NPX : (i + 1) * NPX],
+                scalar=nb[:, c : c + 1],
+                in1=st[("e1", i, c)][:],
+                op0=ALU.mult,
+                op1=ALU.add,
+            )
+
+        def mx_first(i):
+            mx(0, i, 0)
+            mx(0, i, 1)
+            mx(2, i, 0)
 
         def stage_a(i):
             for c in range(CT):
-                e1 = ep.tile([P, NPX], F32, tag="e1", name="e1")
-                gp = ep.tile([P, NPX], F32, tag="gp", name="gp", bufs=4)
-                dd = ep.tile([P, NPX], F32, tag="dd", name="dd")
-                aps = []
-                wps = []
-                for h in range(2):
-                    a_ps = psum.tile([P, BLK], F32, tag="a", name="a_ps")
-                    w_ps = psum.tile([P, BLK], F32, tag="w", name="w_ps")
-                    mx(a_ps, c, i, h)
-                    mx(w_ps, 2 + c, i, h)
-                    aps.append(a_ps)
-                    wps.append(w_ps)
-                for h in range(2):
-                    nc.vector.tensor_tensor(
-                        out=e1[:, h * BLK : (h + 1) * BLK],
-                        in0=aps[h][:],
-                        in1=uh_t[:, i * NPX + h * BLK : i * NPX + (h + 1) * BLK],
-                        op=ALU.add,
-                    )
-                for h in range(2):
-                    nc.vector.scalar_tensor_tensor(
-                        out=gp[:, h * BLK : (h + 1) * BLK],
-                        in0=e1[:, h * BLK : (h + 1) * BLK],
-                        scalar=rr[:, c : c + 1],
-                        in1=wps[h][:],
-                        op0=ALU.mult,
-                        op1=ALU.add,
-                    )
-                nc.vector.scalar_tensor_tensor(
-                    out=dd[:],
-                    in0=uh_t[:, i * NPX : (i + 1) * NPX],
-                    scalar=nb[:, c : c + 1],
-                    in1=e1[:],
-                    op0=ALU.mult,
-                    op1=ALU.add,
-                )
-                st[("gp", i, c)] = gp
-                st[("dd", i, c)] = dd
+                st[("e1", i, c)] = ep.tile([P, NPX], F32, tag="e1", name="e1")
+                st[("gp", i, c)] = ep.tile([P, NPX], F32, tag="gp", name="gp", bufs=4)
+                st[("dd", i, c)] = ep.tile([P, NPX], F32, tag="dd", name="dd")
+                if c == 1:
+                    mx(1, i, 1)
+                    mx(3, i, 0)
+                v1(i, c, 0)
+                if c == 0:
+                    mx(2, i, 1)
+                else:
+                    mx(3, i, 1)
+                v1(i, c, 1)
+                if c == 0:
+                    mx(1, i, 0)
+                v2(i, c, 0)
+                v2(i, c, 1)
+                v3(i, c)
 
-        def stage_sa(i):
-            for c in range(CT):
-                dd = st[("dd", i, c)]
-                nc.scalar.activation(out=dd[:], in_=dd[:], func=ACT.Ln, bias=b2[:, c : c + 1], scale=1.0)
+        def s_ln_d(i, c):
+            dd = st[("dd", i, c)]
+            nc.scalar.activation(out=dd[:], in_=dd[:], func=ACT.Ln, bias=b2[:, c : c + 1], scale=1.0)
 
-        def stage_sb(i):
-            for c in range(CT):
-                dd = st[("dd", i, c)]
-                nc.scalar.activation(out=dd[:], in_=dd[:], func=ACT.Exp, bias=lnk[:, c : c + 1], scale=-1.0)
+        def s_exp(i, c):
+            dd = st[("dd", i, c)]
+            nc.scalar.activation(out=dd[:], in_=dd[:], func=ACT.Exp, bias=lnk[:, c : c + 1], scale=-1.0)
 
         def stage_b(i):
             for c in range(CT):
                 dd = st[("dd", i, c)]
+                gp = st[("gp", i, c)]
                 nc.vector.scalar_tensor_tensor(
                     out=dd[:],
                     in0=dd[:],
@@ -276,65 +307,97 @@ def tile_hyperboliclayer_kernel(tc, z, p, normals, out):
                     op0=ALU.min,
                     op1=ALU.min,
                 )
-            for c in range(CT):
-                gp = st[("gp", i, c)]
-                nc.vector.tensor_tensor(out=gp[:], in0=gp[:], in1=st[("dd", i, c)][:], op=ALU.mult)
+                nc.vector.tensor_tensor(out=gp[:], in0=gp[:], in1=dd[:], op=ALU.mult)
 
-        def stage_sc(i):
-            for c in range(CT):
-                gp = st[("gp", i, c)]
-                q6 = ep.tile([P, NPX], F32, tag="q6", name="q6")
-                xa = ep.tile([P, NPX], F32, tag="xa", name="xa")
-                sg = ep.tile([P, NPX], F32, tag="sg", name="sg")
-                nc.scalar.activation(out=q6[:], in_=gp[:], func=ACT.Square, scale=c2s[:, c : c + 1])
-                nc.scalar.activation(out=xa[:], in_=gp[:], func=ACT.Abs, scale=c2[:, c : c + 1])
-                nc.scalar.activation(out=sg[:], in_=gp[:], func=ACT.Sign)
-                st[("q6", i, c)] = q6
-                st[("xa", i, c)] = xa
-                st[("sg", i, c)] = sg
-            for c in range(CT):
-                lt = ep.tile([P, NPX], F32, tag="lt", name="lt")
-                nc.scalar.activation(out=lt[:], in_=st[("q6", i, c)][:], func=ACT.Sqrt, bias=ones2[:, 0:1], scale=6.0)
-                st[("lt", i, c)] = lt
+        def s_sq_abs(i, c):
+            gp = st[("gp", i, c)]
+            q6 = ep.tile([P, NPX], F32, tag="q6", name="q6")
+            xa = ep.tile([P, NPX], F32, tag="xa", name="xa")
+            sg = ep.tile([P, NPX], F32, tag="sg", name="sg", bufs=3)
+            nc.scalar.activation(out=q6[:], in_=gp[:], func=ACT.Square, scale=c2s[:, c : c + 1])
+            nc.scalar.activation(out=xa[:], in_=gp[:], func=ACT.Abs, scale=c2[:, c : c + 1])
+            nc.scalar.activation(out=sg[:], in_=gp[:], func=ACT.Sign)
+            st[("sg", i, c)] = sg
+            st[("q6", i, c)] = q6
+            st[("xa", i, c)] = xa
 
-        def stage_c(i):
-            for c in range(CT):
-                lt = st[("lt", i, c)]
-                nc.vector.tensor_tensor(out=lt[:], in0=lt[:], in1=st[("xa", i, c)][:], op=ALU.add)
-            for c in range(CT):
-                ns = ep.tile([P, NPX], F32, tag="ns", name="ns")
-                nc.vector.scalar_tensor_tensor(
-                    out=ns[:],
-                    in0=st[("q6", i, c)][:],
-                    scalar=1.0,
-                    in1=st[("xa", i, c)][:],
-                    op0=ALU.subtract,
-                    op1=ALU.mult,
+        def v_pen(i, c):
+            pn = ep.tile([P, NPX], F32, tag="pn", name="pn")
+            nc.vector.tensor_scalar(
+                out=pn[:], in0=st[("q6", i, c)][:], scalar1=KAPPA, scalar2=0.5, op0=ALU.mult, op1=ALU.min
+            )
+            st[("pn", i, c)] = pn
+
+        def s_sqrt(i, c):
+            rt = ep.tile([P, NPX], F32, tag="rt", name="rt")
+            nc.scalar.activation(out=rt[:], in_=st[("q6", i, c)][:], func=ACT.Sqrt, bias=ones2[:, 0:1], scale=6.0)
+            st[("rt", i, c)] = rt
+
+        def pe_t(i, k):
+            c = k // 2
+            h = k % 2
+            xb = ptile("x", "xb")
+            for j in range(4):
+                cols = slice(h * BLK + j * P, h * BLK + (j + 1) * P)
+                for n, key in enumerate(("xa", "rt", "pn")):
+                    nc.tensor.matmul(
+                        out=xb[:, j, :],
+                        lhsT=st[(key, i, c)][:, cols],
+                        rhs=ident_f[:],
+                        is_transpose=True,
+                        start=(n == 0),
+                        stop=(n == 2),
+                    )
+            st[("xb", i, k)] = xb
+
+        def s_ln_t(i, k):
+            c = k // 2
+            h = k % 2
+            if h == 0:
+                st[("lt", i, c)] = ep.tile([P, NPX], F32, tag="lt", name="lt")
+            nc.scalar.activation(
+                out=st[("lt", i, c)][:, hs(h)], in_=flat(st[("xb", i, k)]), func=ACT.Ln, bias=mhalf[:, 0:1], scale=1.0
+            )
+
+        def pe_l(i, k):
+            c = k // 2
+            h = k % 2
+            yb = ptile("y", "yb")
+            for j in range(4):
+                nc.tensor.transpose(
+                    out=yb[:, j, :],
+                    in_=st[("lt", i, c)][:, h * BLK + j * P : h * BLK + (j + 1) * P],
+                    identity=ident_f[:],
                 )
-                st[("ns", i, c)] = ns
+            st[("yb", i, k)] = yb
 
-        def stage_sd(i):
-            for c in range(CT):
-                lt = st[("lt", i, c)]
-                nc.scalar.activation(out=lt[:], in_=lt[:], func=ACT.Ln)
+        def v7(i, c):
+            ns = ep.tile([P, NPX], F32, tag="ns", name="ns")
+            nc.vector.scalar_tensor_tensor(
+                out=ns[:],
+                in0=st[("q6", i, c)][:],
+                scalar=1.0,
+                in1=st[("xa", i, c)][:],
+                op0=ALU.subtract,
+                op1=ALU.mult,
+            )
+            st[("ns", i, c)] = ns
+
+        def v9(i, k):
+            c = k // 2
+            h = k % 2
+            ns = st[("ns", i, c)]
+            nc.vector.scalar_tensor_tensor(
+                out=ns[:, hs(h)], in0=flat(st[("yb", i, k)]), scalar=-1.0, in1=ns[:, hs(h)], op0=ALU.mult, op1=ALU.min
+            )
 
         def stage_d(i):
-            for c in range(CT):
-                lt = st[("lt", i, c)]
-                nc.vector.scalar_tensor_tensor(
-                    out=lt[:], in0=st[("q6", i, c)][:], scalar=THR6, in1=lt[:], op0=ALU.is_ge, op1=ALU.mult
-                )
-            for c in range(CT):
-                lt = st[("lt", i, c)]
-                nc.vector.scalar_tensor_tensor(
-                    out=lt[:], in0=lt[:], scalar=-1.0, in1=st[("ns", i, c)][:], op0=ALU.mult, op1=ALU.min
-                )
             ots = []
             for c in range(CT):
-                ot = ep.tile([P, NPX], F32, tag="ot", name="ot", bufs=4)
+                ot = ep.tile([P, NPX], F32, tag="ot", name="ot", bufs=3)
                 nc.vector.scalar_tensor_tensor(
                     out=ot[:],
-                    in0=st[("lt", i, c)][:],
+                    in0=st[("ns", i, c)][:],
                     scalar=w2[:, c : c + 1],
                     in1=st[("sg", i, c)][:],
                     op0=ALU.mult,
@@ -346,26 +409,84 @@ def tile_hyperboliclayer_kernel(tc, z, p, normals, out):
                 nc.vector.tensor_scalar(out=ot[:], in0=ot[:], scalar1=cap[:, c : c + 1], scalar2=None, op0=ALU.max)
                 nc.sync.dma_start(out=out[i, c * P : (c + 1) * P].rearrange("k h w -> k (h w)"), in_=ot[:])
 
+        def staged(items, n):
+            if n < len(items):
+                comp, dst, blk = items[n]
+                stage_fill(comp, blk)
+
+        def unstage(items, n):
+            if n < len(items):
+                comp, dst, blk = items[n]
+                stage_evac(dst, blk)
+
+        def logs(i):
+            for k in range(4):
+                s_ln_t(i, k)
+                if k < 2:
+                    pe_t(i, k + 2)
+                pe_l(i, k)
+                v9(i, k)
+
         stage_y(0)
-        stage_ev(0)
+        first = [(uh_c, uh_t, 0), (uh_c, uh_t, 1), (s_c, s_t, 2), (s_c, s_t, 3), (rv_c, rv_t, 0), (rv_c, rv_t, 1)]
+        for n in range(2):
+            staged(first, n)
+            unstage(first, n)
+        mx_first(0)
+        for n in range(2, 4):
+            staged(first, n)
+            unstage(first, n)
         stage_a(0)
+        for n in range(4, 6):
+            staged(first, n)
+            unstage(first, n)
         nc.scalar.activation(out=lnk[:], in_=bw5[:], func=ACT.Ln)
         stage_y(1)
+
         for i in range(NB):
+            items = []
+            if i + 1 < NB:
+                items += [(uh_c, uh_t, 2 * i + 2), (uh_c, uh_t, 2 * i + 3)]
+            if i + 2 < NB:
+                items += [(s_c, s_t, 2 * i + 4), (s_c, s_t, 2 * i + 5)]
+            if i + 1 < NB:
+                items += [(rv_c, rv_t, 2 * i + 2), (rv_c, rv_t, 2 * i + 3)]
             if i > 0:
-                stage_sd(i - 1)
-            stage_sa(i)
-            stage_sb(i)
+                logs(i - 1)
+            staged(items, 0)
+            s_ln_d(i, 0)
+            unstage(items, 0)
+            staged(items, 1)
+            s_ln_d(i, 1)
+            unstage(items, 1)
+            if i + 1 < NB:
+                mx_first(i + 1)
+            staged(items, 2)
+            s_exp(i, 0)
+            unstage(items, 2)
+            staged(items, 3)
+            s_exp(i, 1)
+            unstage(items, 3)
             if i > 0:
                 stage_d(i - 1)
-            if i + 1 < NB:
-                stage_ev(i + 1)
             stage_b(i)
-            stage_sc(i)
+            staged(items, 4)
+            s_sq_abs(i, 0)
+            unstage(items, 4)
+            staged(items, 5)
+            s_sq_abs(i, 1)
+            unstage(items, 5)
+            s_sqrt(i, 0)
+            s_sqrt(i, 1)
             if i + 1 < NB:
                 stage_a(i + 1)
+            v_pen(i, 0)
+            v_pen(i, 1)
+            pe_t(i, 0)
+            pe_t(i, 1)
             if i + 2 < NB:
                 stage_y(i + 2)
-            stage_c(i)
-        stage_sd(NB - 1)
+            v7(i, 0)
+            v7(i, 1)
+        logs(NB - 1)
         stage_d(NB - 1)

@@ -22,8 +22,8 @@ D = 512
 FLOPS = 2 * 2 * 256 * D * NB * NPX
 
 A85 = math.log(85.0 + math.sqrt(85.0 * 85.0 + 1.0))
-KAPPA = 30000.0
-NBUF = {"aw": 3, "x": 2, "y": 2, "st": 1}
+THR6 = 0.01 * 0.01 / 6.0
+NBUF = {"aw": 3, "sb": 2, "st": 3}
 
 
 def tile_hyperboliclayer_kernel(tc, z, p, normals, out):
@@ -75,44 +75,54 @@ def tile_hyperboliclayer_kernel(tc, z, p, normals, out):
         c2s = col("c2s")
         w2 = col("w2")
         cap = col("cap")
+        cq = col("cq")
         s_c = keep.tile([P, 32], F32, name="s_c")
         uh_c = keep.tile([P, 32], F32, name="uh_c")
         rv_c = keep.tile([P, 32], F32, name="rv_c")
         uh_t = keep.tile([P, NB * NPX], F32, name="uh_t")
         rv_t = keep.tile([P, NB * NPX], F32, name="rv_t")
-        s_t = keep.tile([P, NB * NPX], F32, name="s_t")
-        mhalf = keep.tile([P, 1], F32, name="mhalf")
-        nc.vector.memset(mhalf[:], -0.5)
 
-        with tc.tile_pool(name="head", bufs=1) as head:
-            wg = head.tile([P, 4, P, 4], BF16, name="wg", align_bytes=64)
-            for i in range(4):
-                raw = p_raw if i < 2 else n_raw
-                src = raw[:, i % 2, :].rearrange("k (q t) -> k t q", t=4)
-                mg = head.tile([P, 4, P], BF16, name="mg%d" % i)
-                if i < 2:
-                    nc.vector.tensor_scalar(out=mg[:], in0=src, scalar1=-1.0, scalar2=None, op0=ALU.mult)
-                else:
-                    nc.vector.tensor_copy(out=mg[:], in_=src)
-                tp = psum.tile([P, 4, P], BF16, tag=("x", "y")[i % 2], name="tp%d" % i)
-                for t in range(4):
-                    nc.tensor.transpose(out=tp[:, t, :], in_=mg[:, t, :], identity=ident_b[:])
-                nc.vector.tensor_copy(out=wg[:, i, :, :], in_=tp[:].rearrange("q t k -> q k t"))
+        wtmp = ctx.enter_context(tc.tile_pool(name="wtmp", bufs=1))
+        wg = wtmp.tile([P, 4, P, 4], BF16, name="wg", align_bytes=64)
+        junk = wtmp.tile([P, D], F32, name="junk")
+        pn_t = wtmp.tile([P, CT, D], F32, name="pn_t")
+        wst = {}
+
+        def w_regroup(i):
+            raw = p_raw if i < 2 else n_raw
+            src = raw[:, i % 2, :].rearrange("k (q t) -> k t q", t=4)
+            mg = wtmp.tile([P, 4, P], BF16, name="mg%d" % i)
+            if i < 2:
+                nc.vector.tensor_scalar(out=mg[:], in0=src, scalar1=-1.0, scalar2=None, op0=ALU.mult)
+            else:
+                nc.vector.tensor_copy(out=mg[:], in_=src)
+            wst[i] = mg
+
+        def w_transpose(i):
+            tp = psum.tile([P, 4, P], BF16, tag="aw", name="tp%d" % i, bufs=NBUF["aw"])
+            for t in range(4):
+                nc.tensor.transpose(out=tp[:, t, :], in_=wst[i][:, t, :], identity=ident_b[:])
+            wst[("tp", i)] = tp
+
+        def w_evac(i):
+            nc.vector.tensor_copy(out=wg[:, i, :, :], in_=wst[("tp", i)][:].rearrange("q t k -> q k t"))
+
+        def w_quant():
             nc.vector.quantize_mx(
-                out=w_codes[:].bitcast(FP8X4),
-                scales=w_scales[:],
-                in_=wg[:].rearrange("q i k t -> q (i k t)"),
+                out=w_codes[:].bitcast(FP8X4), scales=w_scales[:], in_=wg[:].rearrange("q i k t -> q (i k t)")
             )
-            junk = head.tile([P, D], F32, name="junk")
+
+        def cls_sums_s():
             for c in range(CT):
                 nc.scalar.activation(out=junk[:], in_=p_raw[:, c, :], func=ACT.Square, accum_out=ppww[:, c : c + 1])
             for c in range(CT):
                 nc.scalar.activation(
                     out=junk[:], in_=n_raw[:, c, :], func=ACT.Square, accum_out=ppww[:, 2 + c : 3 + c]
                 )
-            pn = head.tile([P, CT, D], F32, name="pn")
-            nc.vector.tensor_tensor(out=pn[:], in0=p_raw[:], in1=n_raw[:], op=ALU.mult)
-            nc.vector.reduce_sum(out=pwp[:], in_=pn[:], axis=AX.X)
+
+        def cls_consts():
+            nc.vector.tensor_tensor(out=pn_t[:], in0=p_raw[:], in1=n_raw[:], op=ALU.mult)
+            nc.vector.reduce_sum(out=pwp[:], in_=pn_t[:], axis=AX.X)
             pp = ppww[:, 0:2]
             ww = ppww[:, 2:4]
             nc.vector.tensor_scalar(out=bc[:], in0=pp, scalar1=-1.0, scalar2=1.0, op0=ALU.mult, op1=ALU.add)
@@ -126,51 +136,20 @@ def tile_hyperboliclayer_kernel(tc, z, p, normals, out):
             nc.vector.reciprocal(out=rw[:], in_=ww)
             nc.vector.tensor_scalar(out=c2[:], in0=rw[:], scalar1=2.0, scalar2=None, op0=ALU.mult)
             nc.vector.tensor_scalar(out=c2s[:], in0=rw[:], scalar1=2.0 / math.sqrt(6.0), scalar2=None, op0=ALU.mult)
+            nc.vector.tensor_tensor(out=cq[:], in0=c2s[:], in1=c2s[:], op=ALU.mult)
             nc.vector.tensor_scalar(out=w2[:], in0=ww, scalar1=2.0, scalar2=None, op0=ALU.mult)
             nc.vector.tensor_scalar(out=cap[:], in0=ww, scalar1=-2.0 * A85, scalar2=None, op0=ALU.mult)
 
-            nsq_c = head.tile([P, 32], F32, name="nsq_c")
-            nts = []
-            for b in range(NB):
-                sq_s = head.tile([P, 2, NPX], F32, name="sqs%d" % b)
-                sq_v = head.tile([P, 2, NPX], F32, name="sqv%d" % b)
-                nc.scalar.activation(out=sq_s[:], in_=zt[b][:, 0:2, :], func=ACT.Square)
-                nc.vector.tensor_tensor(out=sq_v[:], in0=zt[b][:, 2:4, :], in1=zt[b][:, 2:4, :], op=ALU.mult)
-                for hb in range(2):
-                    tg = ("aw", "aw", "aw", "x", "x", "y", "y", "st")[2 * b + hb]
-                    nt = psum.tile([P, 4, P], F32, tag=tg, name="nt", bufs=NBUF[tg])
-                    for c4 in range(4):
-                        c8 = hb * 4 + c4
-                        for j in range(4):
-                            sq = sq_s if j < 2 else sq_v
-                            nc.tensor.matmul(
-                                out=nt[:, c4, :],
-                                lhsT=sq[:, j % 2, c8 * P : (c8 + 1) * P],
-                                rhs=ident_f[:],
-                                is_transpose=True,
-                                start=(j == 0),
-                                stop=(j == 3),
-                            )
-                    nts.append(nt)
-            for k in range(2 * NB):
-                nc.vector.reduce_sum(out=nsq_c[:, 4 * k : 4 * k + 4], in_=nts[k][:], axis=AX.X)
-            nrm = head.tile([P, 32], F32, name="nrm")
-            th = head.tile([P, 32], F32, name="th")
-            rn = head.tile([P, 32], F32, name="rn")
-            zz = head.tile([P, 32], F32, name="zz")
-            vv = head.tile([P, 32], F32, name="vv")
-            nc.vector.tensor_scalar(out=nrm[:], in0=nsq_c[:], scalar1=1.0e-30, scalar2=None, op0=ALU.max)
-            nc.scalar.activation(out=nrm[:], in_=nrm[:], func=ACT.Sqrt)
-            nc.scalar.activation(out=th[:], in_=nrm[:], func=ACT.Tanh)
-            nc.vector.reciprocal(out=rn[:], in_=nrm[:])
-            nc.vector.tensor_tensor(out=s_c[:], in0=th[:], in1=rn[:], op=ALU.mult)
-            nc.vector.tensor_tensor(out=zz[:], in0=th[:], in1=th[:], op=ALU.mult)
-            nc.vector.tensor_scalar(out=uh_c[:], in0=zz[:], scalar1=0.5, scalar2=0.5, op0=ALU.mult, op1=ALU.add)
-            nc.vector.tensor_scalar(out=vv[:], in0=zz[:], scalar1=-1.0, scalar2=1.0, op0=ALU.mult, op1=ALU.add)
-            nc.vector.reciprocal(out=rv_c[:], in_=vv[:])
 
+        sqp = ctx.enter_context(tc.tile_pool(name="sqp", bufs=2))
         ep = ctx.enter_context(tc.tile_pool(name="ep", bufs=2))
         st = {}
+        nsq_c = keep.tile([P, 32], F32, name="nsq_c")
+        nrm = keep.tile([P, 32], F32, name="nrm")
+        th = keep.tile([P, 32], F32, name="th")
+        rn = keep.tile([P, 32], F32, name="rn")
+        zz = keep.tile([P, 32], F32, name="zz")
+        vv = keep.tile([P, 32], F32, name="vv")
 
         def ptile(tg, name):
             return psum.tile([P, 4, P], F32, tag=tg, name=name, bufs=NBUF[tg])
@@ -178,38 +157,99 @@ def tile_hyperboliclayer_kernel(tc, z, p, normals, out):
         def flat(t):
             return t[:].rearrange("q a b -> q (a b)")
 
-        def bcast(dst, comp, blk):
+        def sq_s(b):
+            t = sqp.tile([P, 2, NPX], F32, tag="sqs", name="sqs")
+            nc.scalar.activation(out=t[:], in_=zt[b][:, 0:2, :], func=ACT.Square)
+            st[("sqs", b)] = t
+
+        def sq_v(b):
+            t = sqp.tile([P, 2, NPX], F32, tag="sqv", name="sqv")
+            nc.vector.tensor_tensor(out=t[:], in0=zt[b][:, 2:4, :], in1=zt[b][:, 2:4, :], op=ALU.mult)
+            st[("sqv", b)] = t
+
+        def nt_pe(b, hbs=(0, 1)):
+            for hb in hbs:
+                nt = ptile("sb" if b == 0 else "st", "nt")
+                for c4 in range(4):
+                    c8 = hb * 4 + c4
+                    for j in range(4):
+                        sq = st[("sqs", b)] if j < 2 else st[("sqv", b)]
+                        nc.tensor.matmul(
+                            out=nt[:, c4, :],
+                            lhsT=sq[:, j % 2, c8 * P : (c8 + 1) * P],
+                            rhs=ident_f[:],
+                            is_transpose=True,
+                            start=(j == 0),
+                            stop=(j == 3),
+                        )
+                st[("nt", b, hb)] = nt
+
+        def nt_red(b):
+            for hb in range(2):
+                k = 2 * b + hb
+                nc.vector.reduce_sum(out=nsq_c[:, 4 * k : 4 * k + 4], in_=st[("nt", b, hb)][:], axis=AX.X)
+
+        def chain_v0(lo, hi):
+            nc.vector.tensor_scalar(out=nrm[:, lo:hi], in0=nsq_c[:, lo:hi], scalar1=1.0e-30, scalar2=None, op0=ALU.max)
+
+        def chain_sqrt(lo, hi):
+            nc.scalar.activation(out=nrm[:, lo:hi], in_=nrm[:, lo:hi], func=ACT.Sqrt)
+
+        def chain_tanh(lo, hi):
+            nc.scalar.activation(out=th[:, lo:hi], in_=nrm[:, lo:hi], func=ACT.Tanh)
+
+        def chain_v1(lo, hi):
+            nc.vector.reciprocal(out=rn[:, lo:hi], in_=nrm[:, lo:hi])
+            nc.vector.tensor_tensor(out=s_c[:, lo:hi], in0=th[:, lo:hi], in1=rn[:, lo:hi], op=ALU.mult)
+            nc.vector.tensor_tensor(out=zz[:, lo:hi], in0=th[:, lo:hi], in1=th[:, lo:hi], op=ALU.mult)
+            nc.vector.tensor_scalar(
+                out=uh_c[:, lo:hi], in0=zz[:, lo:hi], scalar1=0.5, scalar2=0.5, op0=ALU.mult, op1=ALU.add
+            )
+            nc.vector.tensor_scalar(
+                out=vv[:, lo:hi], in0=zz[:, lo:hi], scalar1=-1.0, scalar2=1.0, op0=ALU.mult, op1=ALU.add
+            )
+            nc.vector.reciprocal(out=rv_c[:, lo:hi], in_=vv[:, lo:hi])
+
+        def fill(comp, blk, tg="st"):
+            stg = ptile(tg, "stg")
             for j in range(4):
                 cc = blk * 4 + j
                 nc.tensor.transpose(
-                    out=dst[:, j, :], in_=comp[:, cc : cc + 1].to_broadcast([P, P]), identity=ident_f[:]
+                    out=stg[:, j, :], in_=comp[:, cc : cc + 1].to_broadcast([P, P]), identity=ident_f[:]
                 )
+            return stg
 
-        def stage_fill(comp, blk):
-            stg = ptile("st", "stg")
-            bcast(stg, comp, blk)
-            st["stg"] = stg
+        def uh_fill(blk, tg="st"):
+            st["uf"] = fill(uh_c, blk, tg)
 
-        def stage_evac(dst, blk):
-            nc.scalar.copy(out=dst[:, blk * BLK : (blk + 1) * BLK], in_=flat(st["stg"]))
+        def uh_evac(blk):
+            nc.scalar.copy(out=uh_t[:, blk * BLK : (blk + 1) * BLK], in_=flat(st["uf"]))
 
-        def y_mult(i, h, s_ap):
+        def uh_stage(blk, tg="st"):
+            uh_fill(blk, tg)
+            uh_evac(blk)
+
+        def hs(h):
+            return slice(h * BLK, (h + 1) * BLK)
+
+        def rv_stage(blk):
+            stg = fill(rv_c, blk)
+            nc.scalar.copy(out=rv_t[:, blk * BLK : (blk + 1) * BLK], in_=flat(stg))
+
+        def y_fill(i, h):
+            st[("sf", i, h)] = fill(s_c, 2 * i + h, "sb")
+
+        def y_mult(i, h):
+            if h == 0:
+                st[("yg", i)] = ep.tile([P, NPX, 4], BF16, tag="yg", name="yg", align_bytes=64, bufs=1)
             nc.vector.tensor_tensor(
-                out=st[("yg", i)][:, h * BLK : (h + 1) * BLK, :],
-                in0=zt[i][:, :, h * BLK : (h + 1) * BLK].rearrange("q j n -> q n j"),
-                in1=s_ap.unsqueeze(2).to_broadcast([P, BLK, 4]),
+                out=st[("yg", i)][:, hs(h), :],
+                in0=zt[i][:, :, hs(h)].rearrange("q j n -> q n j"),
+                in1=flat(st[("sf", i, h)]).unsqueeze(2).to_broadcast([P, BLK, 4]),
                 op=ALU.mult,
             )
 
-        def stage_y(i):
-            st[("yg", i)] = ep.tile([P, NPX, 4], BF16, tag="yg", name="yg", align_bytes=64, bufs=1)
-            for h in range(2):
-                if i == 0:
-                    sb = ptile("x", "sb")
-                    bcast(sb, s_c, h)
-                    y_mult(i, h, flat(sb))
-                else:
-                    y_mult(i, h, s_t[:, i * NPX + h * BLK : i * NPX + (h + 1) * BLK])
+        def y_quant(i):
             yc = ep.tile([P, NPX], U32, tag="yc", name="yc", align_bytes=64)
             ys = ep.tile([P, NPX], U8, tag="ys", name="ys", align_bytes=64)
             nc.vector.quantize_mx(
@@ -217,7 +257,6 @@ def tile_hyperboliclayer_kernel(tc, z, p, normals, out):
             )
             st[("yc", i)] = yc
             st[("ys", i)] = ys
-
         def mx(op_i, i, h):
             dst = ptile("aw", "mxo")
             nc.tensor.matmul_mx(
@@ -230,9 +269,6 @@ def tile_hyperboliclayer_kernel(tc, z, p, normals, out):
                 stop=True,
             )
             st[("mx", i, op_i, h)] = dst
-
-        def hs(h):
-            return slice(h * BLK, (h + 1) * BLK)
 
         def v1(i, c, h):
             nc.vector.tensor_tensor(
@@ -295,198 +331,184 @@ def tile_hyperboliclayer_kernel(tc, z, p, normals, out):
             dd = st[("dd", i, c)]
             nc.scalar.activation(out=dd[:], in_=dd[:], func=ACT.Exp, bias=lnk[:, c : c + 1], scale=-1.0)
 
-        def stage_b(i):
-            for c in range(CT):
-                dd = st[("dd", i, c)]
-                gp = st[("gp", i, c)]
-                nc.vector.scalar_tensor_tensor(
-                    out=dd[:],
-                    in0=dd[:],
-                    scalar=ke[:, c : c + 1],
-                    in1=rv_t[:, i * NPX : (i + 1) * NPX],
-                    op0=ALU.min,
-                    op1=ALU.min,
-                )
-                nc.vector.tensor_tensor(out=gp[:], in0=gp[:], in1=dd[:], op=ALU.mult)
-
-        def s_sq_abs(i, c):
+        def v45(i, c):
+            dd = st[("dd", i, c)]
             gp = st[("gp", i, c)]
-            q6 = ep.tile([P, NPX], F32, tag="q6", name="q6")
-            xa = ep.tile([P, NPX], F32, tag="xa", name="xa")
-            sg = ep.tile([P, NPX], F32, tag="sg", name="sg", bufs=3)
-            nc.scalar.activation(out=q6[:], in_=gp[:], func=ACT.Square, scale=c2s[:, c : c + 1])
-            nc.scalar.activation(out=xa[:], in_=gp[:], func=ACT.Abs, scale=c2[:, c : c + 1])
-            nc.scalar.activation(out=sg[:], in_=gp[:], func=ACT.Sign)
-            st[("sg", i, c)] = sg
-            st[("q6", i, c)] = q6
-            st[("xa", i, c)] = xa
-
-        def v_pen(i, c):
-            pn = ep.tile([P, NPX], F32, tag="pn", name="pn")
-            nc.vector.tensor_scalar(
-                out=pn[:], in0=st[("q6", i, c)][:], scalar1=KAPPA, scalar2=0.5, op0=ALU.mult, op1=ALU.min
+            nc.vector.scalar_tensor_tensor(
+                out=dd[:],
+                in0=dd[:],
+                scalar=ke[:, c : c + 1],
+                in1=rv_t[:, i * NPX : (i + 1) * NPX],
+                op0=ALU.min,
+                op1=ALU.min,
             )
-            st[("pn", i, c)] = pn
+            nc.vector.tensor_tensor(out=gp[:], in0=gp[:], in1=dd[:], op=ALU.mult)
+
+        def new(tag, i, c):
+            t = ep.tile([P, NPX], F32, tag=tag, name=tag)
+            st[(tag, i, c)] = t
+            return t
+
+        def s_square(i, c):
+            nc.scalar.activation(
+                out=new("q6", i, c)[:], in_=st[("gp", i, c)][:], func=ACT.Square, scale=c2s[:, c : c + 1]
+            )
+
+        def v_square(i, c):
+            gp = st[("gp", i, c)]
+            nc.vector.scalar_tensor_tensor(
+                out=new("q6", i, c)[:], in0=gp[:], scalar=cq[:, c : c + 1], in1=gp[:], op0=ALU.mult, op1=ALU.mult
+            )
+
+        def s_abs(i, c):
+            nc.scalar.activation(out=new("xa", i, c)[:], in_=st[("gp", i, c)][:], func=ACT.Abs, scale=c2[:, c : c + 1])
+
+        def s_sign(i, c):
+            nc.scalar.activation(out=new("sg", i, c)[:], in_=st[("gp", i, c)][:], func=ACT.Sign)
 
         def s_sqrt(i, c):
-            rt = ep.tile([P, NPX], F32, tag="rt", name="rt")
-            nc.scalar.activation(out=rt[:], in_=st[("q6", i, c)][:], func=ACT.Sqrt, bias=ones2[:, 0:1], scale=6.0)
-            st[("rt", i, c)] = rt
-
-        def pe_t(i, k):
-            c = k // 2
-            h = k % 2
-            xb = ptile("x", "xb")
-            for j in range(4):
-                cols = slice(h * BLK + j * P, h * BLK + (j + 1) * P)
-                for n, key in enumerate(("xa", "rt", "pn")):
-                    nc.tensor.matmul(
-                        out=xb[:, j, :],
-                        lhsT=st[(key, i, c)][:, cols],
-                        rhs=ident_f[:],
-                        is_transpose=True,
-                        start=(n == 0),
-                        stop=(n == 2),
-                    )
-            st[("xb", i, k)] = xb
-
-        def s_ln_t(i, k):
-            c = k // 2
-            h = k % 2
-            if h == 0:
-                st[("lt", i, c)] = ep.tile([P, NPX], F32, tag="lt", name="lt")
             nc.scalar.activation(
-                out=st[("lt", i, c)][:, hs(h)], in_=flat(st[("xb", i, k)]), func=ACT.Ln, bias=mhalf[:, 0:1], scale=1.0
+                out=new("lt", i, c)[:], in_=st[("q6", i, c)][:], func=ACT.Sqrt, bias=ones2[:, 0:1], scale=6.0
             )
 
-        def pe_l(i, k):
-            c = k // 2
-            h = k % 2
-            yb = ptile("y", "yb")
-            for j in range(4):
-                nc.tensor.transpose(
-                    out=yb[:, j, :],
-                    in_=st[("lt", i, c)][:, h * BLK + j * P : h * BLK + (j + 1) * P],
-                    identity=ident_f[:],
-                )
-            st[("yb", i, k)] = yb
+        def v6(i, c):
+            lt = st[("lt", i, c)]
+            nc.vector.tensor_tensor(out=lt[:], in0=lt[:], in1=st[("xa", i, c)][:], op=ALU.add)
 
         def v7(i, c):
-            ns = ep.tile([P, NPX], F32, tag="ns", name="ns")
             nc.vector.scalar_tensor_tensor(
-                out=ns[:],
+                out=new("ns", i, c)[:],
                 in0=st[("q6", i, c)][:],
                 scalar=1.0,
                 in1=st[("xa", i, c)][:],
                 op0=ALU.subtract,
                 op1=ALU.mult,
             )
-            st[("ns", i, c)] = ns
 
-        def v9(i, k):
-            c = k // 2
-            h = k % 2
-            ns = st[("ns", i, c)]
+        def s_ln_t(i, c):
+            lt = st[("lt", i, c)]
+            nc.scalar.activation(out=lt[:], in_=lt[:], func=ACT.Ln)
+
+        def v8(i, c):
+            lt = st[("lt", i, c)]
             nc.vector.scalar_tensor_tensor(
-                out=ns[:, hs(h)], in0=flat(st[("yb", i, k)]), scalar=-1.0, in1=ns[:, hs(h)], op0=ALU.mult, op1=ALU.min
+                out=lt[:], in0=st[("q6", i, c)][:], scalar=THR6, in1=lt[:], op0=ALU.is_ge, op1=ALU.mult
             )
 
-        def stage_d(i):
-            ots = []
-            for c in range(CT):
-                ot = ep.tile([P, NPX], F32, tag="ot", name="ot", bufs=3)
-                nc.vector.scalar_tensor_tensor(
-                    out=ot[:],
-                    in0=st[("ns", i, c)][:],
-                    scalar=w2[:, c : c + 1],
-                    in1=st[("sg", i, c)][:],
-                    op0=ALU.mult,
-                    op1=ALU.mult,
-                )
-                ots.append(ot)
-            for c in range(CT):
-                ot = ots[c]
-                nc.vector.tensor_scalar(out=ot[:], in0=ot[:], scalar1=cap[:, c : c + 1], scalar2=None, op0=ALU.max)
-                nc.sync.dma_start(out=out[i, c * P : (c + 1) * P].rearrange("k h w -> k (h w)"), in_=ot[:])
+        def v9(i, c):
+            lt = st[("lt", i, c)]
+            nc.vector.scalar_tensor_tensor(
+                out=lt[:], in0=lt[:], scalar=-1.0, in1=st[("ns", i, c)][:], op0=ALU.mult, op1=ALU.min
+            )
 
-        def staged(items, n):
-            if n < len(items):
-                comp, dst, blk = items[n]
-                stage_fill(comp, blk)
+        def v10(i, c):
+            nc.vector.scalar_tensor_tensor(
+                out=new("ot", i, c)[:],
+                in0=st[("lt", i, c)][:],
+                scalar=w2[:, c : c + 1],
+                in1=st[("sg", i, c)][:],
+                op0=ALU.mult,
+                op1=ALU.mult,
+            )
 
-        def unstage(items, n):
-            if n < len(items):
-                comp, dst, blk = items[n]
-                stage_evac(dst, blk)
+        def v11(i, c):
+            ot = st[("ot", i, c)]
+            nc.vector.tensor_scalar(out=ot[:], in0=ot[:], scalar1=cap[:, c : c + 1], scalar2=None, op0=ALU.max)
+            nc.sync.dma_start(out=out[i, c * P : (c + 1) * P].rearrange("k h w -> k (h w)"), in_=ot[:])
 
-        def logs(i):
-            for k in range(4):
-                s_ln_t(i, k)
-                if k < 2:
-                    pe_t(i, k + 2)
-                pe_l(i, k)
-                v9(i, k)
+        def both(f, i):
+            f(i, 0)
+            f(i, 1)
 
-        stage_y(0)
-        first = [(uh_c, uh_t, 0), (uh_c, uh_t, 1), (s_c, s_t, 2), (s_c, s_t, 3), (rv_c, rv_t, 0), (rv_c, rv_t, 1)]
-        for n in range(2):
-            staged(first, n)
-            unstage(first, n)
+        def stage_y(i):
+            y_fill(i, 0)
+            y_fill(i, 1)
+            y_mult(i, 0)
+            y_mult(i, 1)
+            y_quant(i)
+
+        sq_s(0)
+        sq_v(0)
+        nt_pe(0)
+        sq_s(1)
+        sq_v(1)
+        nt_pe(1)
+        cls_sums_s()
+        for i in range(4):
+            w_regroup(i)
+        nt_red(0)
+        sq_s(2)
+        sq_v(2)
+        for i in range(3):
+            w_transpose(i)
+        for i in range(3):
+            w_evac(i)
+        w_transpose(3)
+        nt_pe(2, (0,))
+        sq_s(3)
+        nt_red(1)
+        nt_pe(2, (1,))
+        chain_v0(0, 16)
+        chain_sqrt(0, 16)
+        chain_tanh(0, 16)
+        sq_v(3)
+        w_evac(3)
+        chain_v1(0, 16)
+        y_fill(0, 0)
+        y_fill(0, 1)
+        nt_pe(3)
+        y_mult(0, 0)
+        nt_red(2)
+        y_mult(0, 1)
+        nt_red(3)
+        chain_v0(16, 32)
+        chain_sqrt(16, 32)
+        chain_tanh(16, 32)
+        y_quant(0)
+        w_quant()
+        cls_consts()
+        for blk in range(2):
+            uh_stage(blk)
         mx_first(0)
-        for n in range(2, 4):
-            staged(first, n)
-            unstage(first, n)
+        for blk in range(2):
+            rv_stage(blk)
         stage_a(0)
-        for n in range(4, 6):
-            staged(first, n)
-            unstage(first, n)
+        chain_v1(16, 32)
         nc.scalar.activation(out=lnk[:], in_=bw5[:], func=ACT.Ln)
         stage_y(1)
 
         for i in range(NB):
-            items = []
-            if i + 1 < NB:
-                items += [(uh_c, uh_t, 2 * i + 2), (uh_c, uh_t, 2 * i + 3)]
-            if i + 2 < NB:
-                items += [(s_c, s_t, 2 * i + 4), (s_c, s_t, 2 * i + 5)]
-            if i + 1 < NB:
-                items += [(rv_c, rv_t, 2 * i + 2), (rv_c, rv_t, 2 * i + 3)]
             if i > 0:
-                logs(i - 1)
-            staged(items, 0)
-            s_ln_d(i, 0)
-            unstage(items, 0)
-            staged(items, 1)
-            s_ln_d(i, 1)
-            unstage(items, 1)
+                both(s_ln_t, i - 1)
+            both(s_ln_d, i)
+            both(s_exp, i)
+            if i > 0:
+                for f in (v8, v9, v10, v11):
+                    both(f, i - 1)
             if i + 1 < NB:
+                for blk in (2 * i + 2, 2 * i + 3):
+                    uh_stage(blk)
                 mx_first(i + 1)
-            staged(items, 2)
-            s_exp(i, 0)
-            unstage(items, 2)
-            staged(items, 3)
-            s_exp(i, 1)
-            unstage(items, 3)
-            if i > 0:
-                stage_d(i - 1)
-            stage_b(i)
-            staged(items, 4)
-            s_sq_abs(i, 0)
-            unstage(items, 4)
-            staged(items, 5)
-            s_sq_abs(i, 1)
-            unstage(items, 5)
-            s_sqrt(i, 0)
-            s_sqrt(i, 1)
+                for blk in (2 * i + 2, 2 * i + 3):
+                    rv_stage(blk)
+            both(v45, i)
+            if i + 1 < NB:
+                for c in range(CT):
+                    s_square(i, c)
+                    s_abs(i, c)
+                    s_sign(i, c)
+                both(s_sqrt, i)
+            else:
+                both(v_square, i)
+                both(s_abs, i)
+                both(s_sqrt, i)
             if i + 1 < NB:
                 stage_a(i + 1)
-            v_pen(i, 0)
-            v_pen(i, 1)
-            pe_t(i, 0)
-            pe_t(i, 1)
             if i + 2 < NB:
                 stage_y(i + 2)
-            v7(i, 0)
-            v7(i, 1)
-        logs(NB - 1)
-        stage_d(NB - 1)
+            both(v6, i)
+            both(v7, i)
+        both(s_ln_t, NB - 1)
+        both(s_sign, NB - 1)
+        for f in (v8, v9, v10, v11):
+            both(f, NB - 1)

@@ -80,7 +80,6 @@ def tile_hyperboliclayer_kernel(tc, z, p, normals, out):
         uh_c = keep.tile([P, 32], F32, name="uh_c")
         rv_c = keep.tile([P, 32], F32, name="rv_c")
         uh_t = keep.tile([P, NB * NPX], F32, name="uh_t")
-        rv_t = keep.tile([P, NB * NPX], F32, name="rv_t")
 
         wtmp = ctx.enter_context(tc.tile_pool(name="wtmp", bufs=1))
         wg = wtmp.tile([P, 4, P, 4], BF16, name="wg", align_bytes=64)
@@ -232,9 +231,9 @@ def tile_hyperboliclayer_kernel(tc, z, p, normals, out):
         def hs(h):
             return slice(h * BLK, (h + 1) * BLK)
 
-        def rv_stage(blk):
-            stg = fill(rv_c, blk)
-            nc.scalar.copy(out=rv_t[:, blk * BLK : (blk + 1) * BLK], in_=flat(stg))
+        def rv_fill(i):
+            for h in range(2):
+                st[("rf", i, h)] = fill(rv_c, 2 * i + h)
 
         def y_fill(i, h):
             st[("sf", i, h)] = fill(s_c, 2 * i + h, "sb")
@@ -288,14 +287,19 @@ def tile_hyperboliclayer_kernel(tc, z, p, normals, out):
                 op1=ALU.add,
             )
 
-        def v3(i, c):
-            nc.vector.scalar_tensor_tensor(
-                out=st[("dd", i, c)][:],
+        def g_hs(i, c):
+            nc.gpsimd.tensor_scalar(
+                out=new("hs", i, c)[:],
                 in0=uh_t[:, i * NPX : (i + 1) * NPX],
-                scalar=nb[:, c : c + 1],
-                in1=st[("e1", i, c)][:],
+                scalar1=nb[:, c : c + 1],
+                scalar2=b2[:, c : c + 1],
                 op0=ALU.mult,
                 op1=ALU.add,
+            )
+
+        def v3(i, c):
+            nc.gpsimd.tensor_tensor(
+                out=st[("dd", i, c)][:], in0=st[("hs", i, c)][:], in1=st[("e1", i, c)][:], op=ALU.add
             )
 
         def mx_first(i):
@@ -325,7 +329,7 @@ def tile_hyperboliclayer_kernel(tc, z, p, normals, out):
 
         def s_ln_d(i, c):
             dd = st[("dd", i, c)]
-            nc.scalar.activation(out=dd[:], in_=dd[:], func=ACT.Ln, bias=b2[:, c : c + 1], scale=1.0)
+            nc.scalar.activation(out=dd[:], in_=dd[:], func=ACT.Ln)
 
         def s_exp(i, c):
             dd = st[("dd", i, c)]
@@ -334,14 +338,15 @@ def tile_hyperboliclayer_kernel(tc, z, p, normals, out):
         def v45(i, c):
             dd = st[("dd", i, c)]
             gp = st[("gp", i, c)]
-            nc.vector.scalar_tensor_tensor(
-                out=dd[:],
-                in0=dd[:],
-                scalar=ke[:, c : c + 1],
-                in1=rv_t[:, i * NPX : (i + 1) * NPX],
-                op0=ALU.min,
-                op1=ALU.min,
-            )
+            for h in range(2):
+                nc.vector.scalar_tensor_tensor(
+                    out=dd[:, hs(h)],
+                    in0=dd[:, hs(h)],
+                    scalar=ke[:, c : c + 1],
+                    in1=flat(st[("rf", i, h)]),
+                    op0=ALU.min,
+                    op1=ALU.min,
+                )
             nc.vector.tensor_tensor(out=gp[:], in0=gp[:], in1=dd[:], op=ALU.mult)
 
         def new(tag, i, c):
@@ -363,8 +368,10 @@ def tile_hyperboliclayer_kernel(tc, z, p, normals, out):
         def s_abs(i, c):
             nc.scalar.activation(out=new("xa", i, c)[:], in_=st[("gp", i, c)][:], func=ACT.Abs, scale=c2[:, c : c + 1])
 
-        def s_sign(i, c):
-            nc.scalar.activation(out=new("sg", i, c)[:], in_=st[("gp", i, c)][:], func=ACT.Sign)
+        def v_sign(i, c):
+            nc.vector.tensor_scalar(
+                out=new("sg", i, c)[:], in0=st[("gp", i, c)][:], scalar1=0.0, scalar2=2.0, op0=ALU.is_ge, op1=ALU.mult
+            )
 
         def s_sqrt(i, c):
             nc.scalar.activation(
@@ -375,15 +382,12 @@ def tile_hyperboliclayer_kernel(tc, z, p, normals, out):
             lt = st[("lt", i, c)]
             nc.vector.tensor_tensor(out=lt[:], in0=lt[:], in1=st[("xa", i, c)][:], op=ALU.add)
 
-        def v7(i, c):
-            nc.vector.scalar_tensor_tensor(
-                out=new("ns", i, c)[:],
-                in0=st[("q6", i, c)][:],
-                scalar=1.0,
-                in1=st[("xa", i, c)][:],
-                op0=ALU.subtract,
-                op1=ALU.mult,
+        def g7(i, c):
+            ns = new("ns", i, c)
+            nc.gpsimd.tensor_scalar(
+                out=ns[:], in0=st[("q6", i, c)][:], scalar1=1.0, scalar2=-1.0, op0=ALU.mult, op1=ALU.add
             )
+            nc.gpsimd.tensor_tensor(out=ns[:], in0=ns[:], in1=st[("xa", i, c)][:], op=ALU.mult)
 
         def s_ln_t(i, c):
             lt = st[("lt", i, c)]
@@ -404,16 +408,18 @@ def tile_hyperboliclayer_kernel(tc, z, p, normals, out):
         def v10(i, c):
             nc.vector.scalar_tensor_tensor(
                 out=new("ot", i, c)[:],
-                in0=st[("lt", i, c)][:],
-                scalar=w2[:, c : c + 1],
-                in1=st[("sg", i, c)][:],
-                op0=ALU.mult,
+                in0=st[("sg", i, c)][:],
+                scalar=1.0,
+                in1=st[("lt", i, c)][:],
+                op0=ALU.subtract,
                 op1=ALU.mult,
             )
 
         def v11(i, c):
             ot = st[("ot", i, c)]
-            nc.vector.tensor_scalar(out=ot[:], in0=ot[:], scalar1=cap[:, c : c + 1], scalar2=None, op0=ALU.max)
+            nc.vector.tensor_scalar(
+                out=ot[:], in0=ot[:], scalar1=w2[:, c : c + 1], scalar2=cap[:, c : c + 1], op0=ALU.mult, op1=ALU.max
+            )
             nc.sync.dma_start(out=out[i, c * P : (c + 1) * P].rearrange("k h w -> k (h w)"), in_=ot[:])
 
         def both(f, i):
@@ -470,8 +476,7 @@ def tile_hyperboliclayer_kernel(tc, z, p, normals, out):
         for blk in range(2):
             uh_stage(blk)
         mx_first(0)
-        for blk in range(2):
-            rv_stage(blk)
+        both(g_hs, 0)
         stage_a(0)
         chain_v1(16, 32)
         nc.scalar.activation(out=lnk[:], in_=bw5[:], func=ACT.Ln)
@@ -480,35 +485,43 @@ def tile_hyperboliclayer_kernel(tc, z, p, normals, out):
         for i in range(NB):
             if i > 0:
                 both(s_ln_t, i - 1)
-            both(s_ln_d, i)
+            if i + 1 < NB:
+                uh_stage(2 * i + 2)
+            s_ln_d(i, 0)
+            if i + 1 < NB:
+                uh_stage(2 * i + 3)
+            s_ln_d(i, 1)
+            rv_fill(i)
             both(s_exp, i)
             if i > 0:
                 for f in (v8, v9, v10, v11):
                     both(f, i - 1)
             if i + 1 < NB:
-                for blk in (2 * i + 2, 2 * i + 3):
-                    uh_stage(blk)
                 mx_first(i + 1)
-                for blk in (2 * i + 2, 2 * i + 3):
-                    rv_stage(blk)
             both(v45, i)
+            both(v_sign, i)
             if i + 1 < NB:
                 for c in range(CT):
                     s_square(i, c)
                     s_abs(i, c)
-                    s_sign(i, c)
+                    g7(i, c)
                 both(s_sqrt, i)
             else:
                 both(v_square, i)
                 both(s_abs, i)
+                both(g7, i)
                 both(s_sqrt, i)
             if i + 1 < NB:
+                both(g_hs, i + 1)
                 stage_a(i + 1)
             if i + 2 < NB:
-                stage_y(i + 2)
+                y_fill(i + 2, 0)
+                y_fill(i + 2, 1)
+                y_mult(i + 2, 0)
+                y_mult(i + 2, 1)
             both(v6, i)
-            both(v7, i)
+            if i + 2 < NB:
+                y_quant(i + 2)
         both(s_ln_t, NB - 1)
-        both(s_sign, NB - 1)
         for f in (v8, v9, v10, v11):
             both(f, NB - 1)

@@ -14,16 +14,19 @@ ACT = mybir.ActivationFunctionType
 AX = mybir.AxisListType
 
 P = 128
+PACK = 4
+D = P * PACK
 NB = 4
 NPX = 1024
 BLK = 512
 CT = 2
-D = 512
-FLOPS = 2 * 2 * 256 * D * NB * NPX
+CHUNKS = NPX // P
+FLOPS = 2 * 2 * CT * P * D * NB * NPX
 
-A85 = math.log(85.0 + math.sqrt(85.0 * 85.0 + 1.0))
-THR6 = 0.01 * 0.01 / 6.0
-NBUF = {"aw": 3, "sb": 2, "st": 3}
+ASINH_85 = math.log(85.0 + math.sqrt(85.0 * 85.0 + 1.0))
+SMALL_Q6 = 0.01 * 0.01 / 6.0
+
+PSUM_BUFS = {"aw": 3, "sb": 2, "st": 3}
 
 
 def tile_hyperboliclayer_kernel(tc, z, p, normals, out):
@@ -37,8 +40,8 @@ def tile_hyperboliclayer_kernel(tc, z, p, normals, out):
         make_identity(nc, ident_b[:])
         ident_f = keep.tile([P, P], F32, name="ident_f")
         make_identity(nc, ident_f[:])
-        ones2 = keep.tile([P, 2], F32, name="ones2")
-        nc.vector.memset(ones2[:], 1.0)
+        one = keep.tile([P, 1], F32, name="one")
+        nc.vector.memset(one[:], 1.0)
 
         p_raw = keep.tile([P, CT, D], BF16, name="p_raw")
         n_raw = keep.tile([P, CT, D], BF16, name="n_raw")
@@ -46,482 +49,464 @@ def tile_hyperboliclayer_kernel(tc, z, p, normals, out):
         nc.scalar.dma_start(out=n_raw[:], in_=normals.rearrange("(c k) d -> k c d", k=P))
         zt = []
         for b in range(NB):
-            zb = keep.tile([P, 4, NPX], BF16, name="z%d" % b)
-            nc.sync.dma_start(out=zb[:], in_=z[b].rearrange("(q j) h w -> q j (h w)", j=4))
+            zb = keep.tile([P, PACK, NPX], BF16, name="z%d" % b)
+            nc.sync.dma_start(out=zb[:], in_=z[b].rearrange("(q j) h w -> q j (h w)", j=PACK))
             zt.append(zb)
 
         warm = keep.tile([P, 1], F32, name="warm")
-        nc.scalar.activation(out=warm[:], in_=ones2[:, 0:1], func=ACT.Sqrt)
+        nc.scalar.activation(out=warm[:], in_=one[:], func=ACT.Sqrt)
 
         w_codes = keep.tile([P, 4 * P], U32, name="w_codes", align_bytes=64)
         w_scales = keep.tile([P, 4 * P], U8, name="w_scales", align_bytes=64)
-        ppww = keep.tile([P, 4], F32, name="ppww")
+        ppww = keep.tile([P, 2 * CT], F32, name="ppww")
         pwp = keep.tile([P, CT], F32, name="pwp")
 
-        def col(name):
+        def per_class(name):
             return keep.tile([P, CT], F32, name=name)
 
-        bc = col("bc")
-        rb = col("rb")
-        rr = col("rr")
-        nb = col("nb")
-        b2 = col("b2")
-        bw = col("bw")
-        ke = col("ke")
-        bw5 = col("bw5")
-        lnk = col("lnk")
-        rw = col("rw")
-        c2 = col("c2")
-        c2s = col("c2s")
-        w2 = col("w2")
-        cap = col("cap")
-        cq = col("cq")
-        s_c = keep.tile([P, 32], F32, name="s_c")
-        uh_c = keep.tile([P, 32], F32, name="uh_c")
-        rv_c = keep.tile([P, 32], F32, name="rv_c")
+        b_c = per_class("b_c")
+        rb_c = per_class("rb_c")
+        r_c = per_class("r_c")
+        nb_c = per_class("nb_c")
+        hb_c = per_class("hb_c")
+        bw_c = per_class("bw_c")
+        kcap_c = per_class("kcap_c")
+        k_c = per_class("k_c")
+        lnk_c = per_class("lnk_c")
+        rw_c = per_class("rw_c")
+        x_c = per_class("x_c")
+        xq_c = per_class("xq_c")
+        w2_c = per_class("w2_c")
+        cap_c = per_class("cap_c")
+        xqq_c = per_class("xqq_c")
+
+        s_px = keep.tile([P, NB * CHUNKS], F32, name="s_px")
+        uh_px = keep.tile([P, NB * CHUNKS], F32, name="uh_px")
+        rv_px = keep.tile([P, NB * CHUNKS], F32, name="rv_px")
+        nsq_px = keep.tile([P, NB * CHUNKS], F32, name="nsq_px")
+        n_px = keep.tile([P, NB * CHUNKS], F32, name="n_px")
+        th_px = keep.tile([P, NB * CHUNKS], F32, name="th_px")
+        rn_px = keep.tile([P, NB * CHUNKS], F32, name="rn_px")
+        zz_px = keep.tile([P, NB * CHUNKS], F32, name="zz_px")
+        v_px = keep.tile([P, NB * CHUNKS], F32, name="v_px")
         uh_t = keep.tile([P, NB * NPX], F32, name="uh_t")
+        rv_t = keep.tile([P, NB * NPX], F32, name="rv_t")
 
         wtmp = ctx.enter_context(tc.tile_pool(name="wtmp", bufs=1))
-        wg = wtmp.tile([P, 4, P, 4], BF16, name="wg", align_bytes=64)
-        junk = wtmp.tile([P, D], F32, name="junk")
-        pn_t = wtmp.tile([P, CT, D], F32, name="pn_t")
-        wst = {}
-
-        def w_regroup(i):
-            raw = p_raw if i < 2 else n_raw
-            src = raw[:, i % 2, :].rearrange("k (q t) -> k t q", t=4)
-            mg = wtmp.tile([P, 4, P], BF16, name="mg%d" % i)
-            if i < 2:
-                nc.vector.tensor_scalar(out=mg[:], in0=src, scalar1=-1.0, scalar2=None, op0=ALU.mult)
-            else:
-                nc.vector.tensor_copy(out=mg[:], in_=src)
-            wst[i] = mg
-
-        def w_transpose(i):
-            tp = psum.tile([P, 4, P], BF16, tag="aw", name="tp%d" % i, bufs=NBUF["aw"])
-            for t in range(4):
-                nc.tensor.transpose(out=tp[:, t, :], in_=wst[i][:, t, :], identity=ident_b[:])
-            wst[("tp", i)] = tp
-
-        def w_evac(i):
-            nc.vector.tensor_copy(out=wg[:, i, :, :], in_=wst[("tp", i)][:].rearrange("q t k -> q k t"))
-
-        def w_quant():
-            nc.vector.quantize_mx(
-                out=w_codes[:].bitcast(FP8X4), scales=w_scales[:], in_=wg[:].rearrange("q i k t -> q (i k t)")
-            )
-
-        def cls_sums_s():
-            for c in range(CT):
-                nc.scalar.activation(out=junk[:], in_=p_raw[:, c, :], func=ACT.Square, accum_out=ppww[:, c : c + 1])
-            for c in range(CT):
-                nc.scalar.activation(
-                    out=junk[:], in_=n_raw[:, c, :], func=ACT.Square, accum_out=ppww[:, 2 + c : 3 + c]
-                )
-
-        def cls_consts():
-            nc.vector.tensor_tensor(out=pn_t[:], in0=p_raw[:], in1=n_raw[:], op=ALU.mult)
-            nc.vector.reduce_sum(out=pwp[:], in_=pn_t[:], axis=AX.X)
-            pp = ppww[:, 0:2]
-            ww = ppww[:, 2:4]
-            nc.vector.tensor_scalar(out=bc[:], in0=pp, scalar1=-1.0, scalar2=1.0, op0=ALU.mult, op1=ALU.add)
-            nc.vector.reciprocal(out=rb[:], in_=bc[:])
-            nc.vector.scalar_tensor_tensor(out=rr[:], in0=pwp[:], scalar=-2.0, in1=rb[:], op0=ALU.mult, op1=ALU.mult)
-            nc.vector.tensor_scalar(out=nb[:], in0=bc[:], scalar1=-1.0, scalar2=None, op0=ALU.mult)
-            nc.vector.tensor_scalar(out=b2[:], in0=bc[:], scalar1=0.5, scalar2=None, op0=ALU.mult)
-            nc.vector.tensor_tensor(out=bw[:], in0=bc[:], in1=ww, op=ALU.mult)
-            nc.vector.tensor_scalar(out=ke[:], in0=bw[:], scalar1=1.0e10, scalar2=None, op0=ALU.mult)
-            nc.vector.tensor_scalar(out=bw5[:], in0=bw[:], scalar1=0.5e5, scalar2=None, op0=ALU.mult)
-            nc.vector.reciprocal(out=rw[:], in_=ww)
-            nc.vector.tensor_scalar(out=c2[:], in0=rw[:], scalar1=2.0, scalar2=None, op0=ALU.mult)
-            nc.vector.tensor_scalar(out=c2s[:], in0=rw[:], scalar1=2.0 / math.sqrt(6.0), scalar2=None, op0=ALU.mult)
-            nc.vector.tensor_tensor(out=cq[:], in0=c2s[:], in1=c2s[:], op=ALU.mult)
-            nc.vector.tensor_scalar(out=w2[:], in0=ww, scalar1=2.0, scalar2=None, op0=ALU.mult)
-            nc.vector.tensor_scalar(out=cap[:], in0=ww, scalar1=-2.0 * A85, scalar2=None, op0=ALU.mult)
-
-
         sqp = ctx.enter_context(tc.tile_pool(name="sqp", bufs=2))
         ep = ctx.enter_context(tc.tile_pool(name="ep", bufs=2))
-        st = {}
-        nsq_c = keep.tile([P, 32], F32, name="nsq_c")
-        nrm = keep.tile([P, 32], F32, name="nrm")
-        th = keep.tile([P, 32], F32, name="th")
-        rn = keep.tile([P, 32], F32, name="rn")
-        zz = keep.tile([P, 32], F32, name="zz")
-        vv = keep.tile([P, 32], F32, name="vv")
+        live = {}
 
-        def ptile(tg, name):
-            return psum.tile([P, 4, P], F32, tag=tg, name=name, bufs=NBUF[tg])
+        def bank(tag):
+            return psum.tile([P, 4, P], F32, tag=tag, name=tag, bufs=PSUM_BUFS[tag])
 
         def flat(t):
             return t[:].rearrange("q a b -> q (a b)")
 
-        def sq_s(b):
-            t = sqp.tile([P, 2, NPX], F32, tag="sqs", name="sqs")
-            nc.scalar.activation(out=t[:], in_=zt[b][:, 0:2, :], func=ACT.Square)
-            st[("sqs", b)] = t
-
-        def sq_v(b):
-            t = sqp.tile([P, 2, NPX], F32, tag="sqv", name="sqv")
-            nc.vector.tensor_tensor(out=t[:], in0=zt[b][:, 2:4, :], in1=zt[b][:, 2:4, :], op=ALU.mult)
-            st[("sqv", b)] = t
-
-        def nt_pe(b, hbs=(0, 1)):
-            for hb in hbs:
-                nt = ptile("sb" if b == 0 else "st", "nt")
-                for c4 in range(4):
-                    c8 = hb * 4 + c4
-                    for j in range(4):
-                        sq = st[("sqs", b)] if j < 2 else st[("sqv", b)]
-                        nc.tensor.matmul(
-                            out=nt[:, c4, :],
-                            lhsT=sq[:, j % 2, c8 * P : (c8 + 1) * P],
-                            rhs=ident_f[:],
-                            is_transpose=True,
-                            start=(j == 0),
-                            stop=(j == 3),
-                        )
-                st[("nt", b, hb)] = nt
-
-        def nt_red(b):
-            for hb in range(2):
-                k = 2 * b + hb
-                nc.vector.reduce_sum(out=nsq_c[:, 4 * k : 4 * k + 4], in_=st[("nt", b, hb)][:], axis=AX.X)
-
-        def chain_v0(lo, hi):
-            nc.vector.tensor_scalar(out=nrm[:, lo:hi], in0=nsq_c[:, lo:hi], scalar1=1.0e-30, scalar2=None, op0=ALU.max)
-
-        def chain_sqrt(lo, hi):
-            nc.scalar.activation(out=nrm[:, lo:hi], in_=nrm[:, lo:hi], func=ACT.Sqrt)
-
-        def chain_tanh(lo, hi):
-            nc.scalar.activation(out=th[:, lo:hi], in_=nrm[:, lo:hi], func=ACT.Tanh)
-
-        def chain_v1(lo, hi):
-            nc.vector.reciprocal(out=rn[:, lo:hi], in_=nrm[:, lo:hi])
-            nc.vector.tensor_tensor(out=s_c[:, lo:hi], in0=th[:, lo:hi], in1=rn[:, lo:hi], op=ALU.mult)
-            nc.vector.tensor_tensor(out=zz[:, lo:hi], in0=th[:, lo:hi], in1=th[:, lo:hi], op=ALU.mult)
-            nc.vector.tensor_scalar(
-                out=uh_c[:, lo:hi], in0=zz[:, lo:hi], scalar1=0.5, scalar2=0.5, op0=ALU.mult, op1=ALU.add
-            )
-            nc.vector.tensor_scalar(
-                out=vv[:, lo:hi], in0=zz[:, lo:hi], scalar1=-1.0, scalar2=1.0, op0=ALU.mult, op1=ALU.add
-            )
-            nc.vector.reciprocal(out=rv_c[:, lo:hi], in_=vv[:, lo:hi])
-
-        def fill(comp, blk, tg="st"):
-            stg = ptile(tg, "stg")
-            for j in range(4):
-                cc = blk * 4 + j
-                nc.tensor.transpose(
-                    out=stg[:, j, :], in_=comp[:, cc : cc + 1].to_broadcast([P, P]), identity=ident_f[:]
-                )
-            return stg
-
-        def uh_fill(blk, tg="st"):
-            st["uf"] = fill(uh_c, blk, tg)
-
-        def uh_evac(blk):
-            nc.scalar.copy(out=uh_t[:, blk * BLK : (blk + 1) * BLK], in_=flat(st["uf"]))
-
-        def uh_stage(blk, tg="st"):
-            uh_fill(blk, tg)
-            uh_evac(blk)
-
-        def hs(h):
+        def half(h):
             return slice(h * BLK, (h + 1) * BLK)
 
-        def rv_fill(i):
+        def unit(tag, i, c):
+            t = ep.tile([P, NPX], F32, tag=tag, name=tag)
+            live[(tag, i, c)] = t
+            return t
+
+        def both(stage, i):
+            stage(i, 0)
+            stage(i, 1)
+
+        w_grouped = wtmp.tile([P, 4, P, PACK], BF16, name="w_grouped", align_bytes=64)
+        sq_junk = wtmp.tile([P, D], F32, name="sq_junk")
+        pn_t = wtmp.tile([P, CT, D], F32, name="pn_t")
+
+        def w_sort(i):
+            raw = p_raw if i < CT else n_raw
+            src = raw[:, i % CT, :].rearrange("k (q t) -> k t q", t=PACK)
+            srt = wtmp.tile([P, PACK, P], BF16, name="w_sorted%d" % i)
+            if i < CT:
+                nc.vector.tensor_scalar(out=srt[:], in0=src, scalar1=-1.0, scalar2=None, op0=ALU.mult)
+            else:
+                nc.vector.tensor_copy(out=srt[:], in_=src)
+            live[("w_sorted", i)] = srt
+
+        def w_transpose(i):
+            tp = psum.tile([P, PACK, P], BF16, tag="aw", name="w_t%d" % i, bufs=PSUM_BUFS["aw"])
+            for t in range(PACK):
+                nc.tensor.transpose(out=tp[:, t, :], in_=live[("w_sorted", i)][:, t, :], identity=ident_b[:])
+            live[("w_t", i)] = tp
+
+        def w_group(i):
+            nc.vector.tensor_copy(out=w_grouped[:, i, :, :], in_=live[("w_t", i)][:].rearrange("q t k -> q k t"))
+
+        def w_quantise():
+            nc.vector.quantize_mx(
+                out=w_codes[:].bitcast(FP8X4), scales=w_scales[:], in_=w_grouped[:].rearrange("q i k t -> q (i k t)")
+            )
+
+        def class_sums():
+            for c in range(CT):
+                nc.scalar.activation(
+                    out=sq_junk[:], in_=p_raw[:, c, :], func=ACT.Square, accum_out=ppww[:, c : c + 1]
+                )
+            for c in range(CT):
+                nc.scalar.activation(
+                    out=sq_junk[:], in_=n_raw[:, c, :], func=ACT.Square, accum_out=ppww[:, CT + c : CT + c + 1]
+                )
+
+        def class_constants():
+            def scaled(dst, src, factor):
+                nc.vector.tensor_scalar(out=dst[:], in0=src, scalar1=factor, scalar2=None, op0=ALU.mult)
+
+            pp = ppww[:, 0:CT]
+            ww = ppww[:, CT : 2 * CT]
+            nc.vector.tensor_tensor(out=pn_t[:], in0=p_raw[:], in1=n_raw[:], op=ALU.mult)
+            nc.vector.reduce_sum(out=pwp[:], in_=pn_t[:], axis=AX.X)
+            nc.vector.tensor_scalar(out=b_c[:], in0=pp, scalar1=-1.0, scalar2=1.0, op0=ALU.mult, op1=ALU.add)
+            nc.vector.reciprocal(out=rb_c[:], in_=b_c[:])
+            nc.vector.scalar_tensor_tensor(
+                out=r_c[:], in0=pwp[:], scalar=-2.0, in1=rb_c[:], op0=ALU.mult, op1=ALU.mult
+            )
+            scaled(nb_c, b_c[:], -1.0)
+            scaled(hb_c, b_c[:], 0.5)
+            nc.vector.tensor_tensor(out=bw_c[:], in0=b_c[:], in1=ww, op=ALU.mult)
+            scaled(kcap_c, bw_c[:], 1.0e10)
+            scaled(k_c, bw_c[:], 0.5e5)
+            nc.vector.reciprocal(out=rw_c[:], in_=ww)
+            scaled(x_c, rw_c[:], 2.0)
+            scaled(xq_c, rw_c[:], 2.0 / math.sqrt(6.0))
+            nc.vector.tensor_tensor(out=xqq_c[:], in0=xq_c[:], in1=xq_c[:], op=ALU.mult)
+            scaled(w2_c, ww, 2.0)
+            scaled(cap_c, ww, -2.0 * ASINH_85)
+
+        def square_s(b):
+            t = sqp.tile([P, 2, NPX], F32, tag="sq_s", name="sq_s")
+            nc.scalar.activation(out=t[:], in_=zt[b][:, 0:2, :], func=ACT.Square)
+            live[("sq_s", b)] = t
+
+        def square_v(b):
+            t = sqp.tile([P, 2, NPX], F32, tag="sq_v", name="sq_v")
+            nc.vector.tensor_tensor(out=t[:], in0=zt[b][:, 2:4, :], in1=zt[b][:, 2:4, :], op=ALU.mult)
+            live[("sq_v", b)] = t
+
+        def norm_transpose(b, h):
+            nt = bank("sb" if b == 0 else "st")
+            for c4 in range(4):
+                cols = slice((4 * h + c4) * P, (4 * h + c4 + 1) * P)
+                for j in range(PACK):
+                    sq = live[("sq_s", b)] if j < 2 else live[("sq_v", b)]
+                    nc.tensor.matmul(
+                        out=nt[:, c4, :],
+                        lhsT=sq[:, j % 2, cols],
+                        rhs=ident_f[:],
+                        is_transpose=True,
+                        start=(j == 0),
+                        stop=(j == PACK - 1),
+                    )
+            live[("nt", b, h)] = nt
+
+        def norm_reduce(b):
             for h in range(2):
-                st[("rf", i, h)] = fill(rv_c, 2 * i + h)
+                k = CHUNKS * b + 4 * h
+                nc.vector.reduce_sum(out=nsq_px[:, k : k + 4], in_=live[("nt", b, h)][:], axis=AX.X)
 
-        def y_fill(i, h):
-            st[("sf", i, h)] = fill(s_c, 2 * i + h, "sb")
+        def px(t, b0, b1):
+            return t[:, CHUNKS * b0 : CHUNKS * b1]
 
-        def y_mult(i, h):
+        def pixel_floor(b0, b1):
+            nc.vector.tensor_scalar(
+                out=px(n_px, b0, b1), in0=px(nsq_px, b0, b1), scalar1=1.0e-30, scalar2=None, op0=ALU.max
+            )
+
+        def pixel_sqrt(b0, b1):
+            nc.scalar.activation(out=px(n_px, b0, b1), in_=px(n_px, b0, b1), func=ACT.Sqrt)
+
+        def pixel_tanh(b0, b1):
+            nc.scalar.activation(out=px(th_px, b0, b1), in_=px(n_px, b0, b1), func=ACT.Tanh)
+
+        def pixel_values(b0, b1):
+            th = px(th_px, b0, b1)
+            zz = px(zz_px, b0, b1)
+            nc.vector.reciprocal(out=px(rn_px, b0, b1), in_=px(n_px, b0, b1))
+            nc.vector.tensor_tensor(out=px(s_px, b0, b1), in0=th, in1=px(rn_px, b0, b1), op=ALU.mult)
+            nc.vector.tensor_tensor(out=zz, in0=th, in1=th, op=ALU.mult)
+            nc.vector.tensor_scalar(out=px(uh_px, b0, b1), in0=zz, scalar1=0.5, scalar2=0.5, op0=ALU.mult, op1=ALU.add)
+            nc.vector.tensor_scalar(out=px(v_px, b0, b1), in0=zz, scalar1=-1.0, scalar2=1.0, op0=ALU.mult, op1=ALU.add)
+            nc.vector.reciprocal(out=px(rv_px, b0, b1), in_=px(v_px, b0, b1))
+
+        def spread(values, i, h, tag):
+            t = bank(tag)
+            for j in range(4):
+                col = CHUNKS * i + 4 * h + j
+                nc.tensor.transpose(
+                    out=t[:, j, :], in_=values[:, col : col + 1].to_broadcast([P, P]), identity=ident_f[:]
+                )
+            return t
+
+        def spread_to_sbuf(values, dst, i):
+            for h in range(2):
+                t = spread(values, i, h, "st")
+                nc.scalar.copy(out=dst[:, i * NPX + h * BLK : i * NPX + (h + 1) * BLK], in_=flat(t))
+
+        def y_spread(i):
+            for h in range(2):
+                live[("s", i, h)] = spread(s_px, i, h, "sb")
+
+        def y_scale(i, h):
             if h == 0:
-                st[("yg", i)] = ep.tile([P, NPX, 4], BF16, tag="yg", name="yg", align_bytes=64, bufs=1)
+                live[("y", i)] = ep.tile([P, NPX, PACK], BF16, tag="y", name="y", align_bytes=64, bufs=1)
             nc.vector.tensor_tensor(
-                out=st[("yg", i)][:, hs(h), :],
-                in0=zt[i][:, :, hs(h)].rearrange("q j n -> q n j"),
-                in1=flat(st[("sf", i, h)]).unsqueeze(2).to_broadcast([P, BLK, 4]),
+                out=live[("y", i)][:, half(h), :],
+                in0=zt[i][:, :, half(h)].rearrange("q j n -> q n j"),
+                in1=flat(live[("s", i, h)]).unsqueeze(2).to_broadcast([P, BLK, PACK]),
                 op=ALU.mult,
             )
 
-        def y_quant(i):
-            yc = ep.tile([P, NPX], U32, tag="yc", name="yc", align_bytes=64)
-            ys = ep.tile([P, NPX], U8, tag="ys", name="ys", align_bytes=64)
+        def y_quantise(i):
+            codes = ep.tile([P, NPX], U32, tag="y_codes", name="y_codes", align_bytes=64)
+            scales = ep.tile([P, NPX], U8, tag="y_scales", name="y_scales", align_bytes=64)
             nc.vector.quantize_mx(
-                out=yc[:].bitcast(FP8X4), scales=ys[:], in_=st[("yg", i)][:].rearrange("q n j -> q (n j)")
+                out=codes[:].bitcast(FP8X4), scales=scales[:], in_=live[("y", i)][:].rearrange("q n j -> q (n j)")
             )
-            st[("yc", i)] = yc
-            st[("ys", i)] = ys
-        def mx(op_i, i, h):
-            dst = ptile("aw", "mxo")
+            live[("y_codes", i)] = codes
+            live[("y_scales", i)] = scales
+
+        def stage_y(i):
+            y_spread(i)
+            y_scale(i, 0)
+            y_scale(i, 1)
+            y_quantise(i)
+
+        def mx(operand, i, h):
+            acc = bank("aw")
             nc.tensor.matmul_mx(
-                out=flat(dst),
-                lhsT=w_codes[:, op_i * P : (op_i + 1) * P].bitcast(FP8X4),
-                lhsT_scale=w_scales[:, op_i * P : (op_i + 1) * P],
-                rhs=st[("yc", i)][:, h * BLK : (h + 1) * BLK].bitcast(FP8X4),
-                rhs_scale=st[("ys", i)][:, h * BLK : (h + 1) * BLK],
+                out=flat(acc),
+                lhsT=w_codes[:, operand * P : (operand + 1) * P].bitcast(FP8X4),
+                lhsT_scale=w_scales[:, operand * P : (operand + 1) * P],
+                rhs=live[("y_codes", i)][:, half(h)].bitcast(FP8X4),
+                rhs_scale=live[("y_scales", i)][:, half(h)],
                 start=True,
                 stop=True,
             )
-            st[("mx", i, op_i, h)] = dst
+            live[("mx", i, operand, h)] = acc
 
-        def v1(i, c, h):
+        def e_add(i, c, h):
             nc.vector.tensor_tensor(
-                out=st[("e1", i, c)][:, hs(h)],
-                in0=flat(st[("mx", i, c, h)]),
+                out=live[("e", i, c)][:, half(h)],
+                in0=flat(live[("mx", i, c, h)]),
                 in1=uh_t[:, i * NPX + h * BLK : i * NPX + (h + 1) * BLK],
                 op=ALU.add,
             )
 
-        def v2(i, c, h):
+        def g_form(i, c, h):
             nc.vector.scalar_tensor_tensor(
-                out=st[("gp", i, c)][:, hs(h)],
-                in0=st[("e1", i, c)][:, hs(h)],
-                scalar=rr[:, c : c + 1],
-                in1=flat(st[("mx", i, 2 + c, h)]),
+                out=live[("g", i, c)][:, half(h)],
+                in0=live[("e", i, c)][:, half(h)],
+                scalar=r_c[:, c : c + 1],
+                in1=flat(live[("mx", i, CT + c, h)]),
                 op0=ALU.mult,
                 op1=ALU.add,
             )
 
-        def g_hs(i, c):
-            nc.gpsimd.tensor_scalar(
-                out=new("hs", i, c)[:],
+        def den_form(i, c):
+            nc.vector.scalar_tensor_tensor(
+                out=live[("k", i, c)][:],
                 in0=uh_t[:, i * NPX : (i + 1) * NPX],
-                scalar1=nb[:, c : c + 1],
-                scalar2=b2[:, c : c + 1],
+                scalar=nb_c[:, c : c + 1],
+                in1=live[("e", i, c)][:],
                 op0=ALU.mult,
                 op1=ALU.add,
             )
 
-        def v3(i, c):
-            nc.gpsimd.tensor_tensor(
-                out=st[("dd", i, c)][:], in0=st[("hs", i, c)][:], in1=st[("e1", i, c)][:], op=ALU.add
-            )
-
-        def mx_first(i):
+        def mx_ahead(i):
             mx(0, i, 0)
             mx(0, i, 1)
-            mx(2, i, 0)
+            mx(CT, i, 0)
 
-        def stage_a(i):
+        def stage_front(i):
             for c in range(CT):
-                st[("e1", i, c)] = ep.tile([P, NPX], F32, tag="e1", name="e1")
-                st[("gp", i, c)] = ep.tile([P, NPX], F32, tag="gp", name="gp", bufs=4)
-                st[("dd", i, c)] = ep.tile([P, NPX], F32, tag="dd", name="dd")
+                unit("e", i, c)
+                live[("g", i, c)] = ep.tile([P, NPX], F32, tag="g", name="g", bufs=4)
+                unit("k", i, c)
                 if c == 1:
                     mx(1, i, 1)
-                    mx(3, i, 0)
-                v1(i, c, 0)
-                if c == 0:
-                    mx(2, i, 1)
-                else:
-                    mx(3, i, 1)
-                v1(i, c, 1)
+                    mx(CT + 1, i, 0)
+                e_add(i, c, 0)
+                mx(CT + c, i, 1)
+                e_add(i, c, 1)
                 if c == 0:
                     mx(1, i, 0)
-                v2(i, c, 0)
-                v2(i, c, 1)
-                v3(i, c)
+                g_form(i, c, 0)
+                g_form(i, c, 1)
+                den_form(i, c)
 
-        def s_ln_d(i, c):
-            dd = st[("dd", i, c)]
-            nc.scalar.activation(out=dd[:], in_=dd[:], func=ACT.Ln)
+        def den_ln(i, c):
+            k = live[("k", i, c)]
+            nc.scalar.activation(out=k[:], in_=k[:], func=ACT.Ln, bias=hb_c[:, c : c + 1], scale=1.0)
 
-        def s_exp(i, c):
-            dd = st[("dd", i, c)]
-            nc.scalar.activation(out=dd[:], in_=dd[:], func=ACT.Exp, bias=lnk[:, c : c + 1], scale=-1.0)
+        def den_exp(i, c):
+            k = live[("k", i, c)]
+            nc.scalar.activation(out=k[:], in_=k[:], func=ACT.Exp, bias=lnk_c[:, c : c + 1], scale=-1.0)
 
-        def v45(i, c):
-            dd = st[("dd", i, c)]
-            gp = st[("gp", i, c)]
-            for h in range(2):
-                nc.vector.scalar_tensor_tensor(
-                    out=dd[:, hs(h)],
-                    in0=dd[:, hs(h)],
-                    scalar=ke[:, c : c + 1],
-                    in1=flat(st[("rf", i, h)]),
-                    op0=ALU.min,
-                    op1=ALU.min,
-                )
-            nc.vector.tensor_tensor(out=gp[:], in0=gp[:], in1=dd[:], op=ALU.mult)
+        def g_clamp(i, c):
+            k = live[("k", i, c)]
+            g = live[("g", i, c)]
+            nc.vector.scalar_tensor_tensor(
+                out=k[:],
+                in0=k[:],
+                scalar=kcap_c[:, c : c + 1],
+                in1=rv_t[:, i * NPX : (i + 1) * NPX],
+                op0=ALU.min,
+                op1=ALU.min,
+            )
+            nc.vector.tensor_tensor(out=g[:], in0=g[:], in1=k[:], op=ALU.mult)
 
-        def new(tag, i, c):
-            t = ep.tile([P, NPX], F32, tag=tag, name=tag)
-            st[(tag, i, c)] = t
-            return t
-
-        def s_square(i, c):
+        def q_scalar(i, c):
             nc.scalar.activation(
-                out=new("q6", i, c)[:], in_=st[("gp", i, c)][:], func=ACT.Square, scale=c2s[:, c : c + 1]
+                out=unit("q6", i, c)[:], in_=live[("g", i, c)][:], func=ACT.Square, scale=xq_c[:, c : c + 1]
             )
 
-        def v_square(i, c):
-            gp = st[("gp", i, c)]
+        def q_vector(i, c):
+            g = live[("g", i, c)]
             nc.vector.scalar_tensor_tensor(
-                out=new("q6", i, c)[:], in0=gp[:], scalar=cq[:, c : c + 1], in1=gp[:], op0=ALU.mult, op1=ALU.mult
+                out=unit("q6", i, c)[:], in0=g[:], scalar=xqq_c[:, c : c + 1], in1=g[:], op0=ALU.mult, op1=ALU.mult
             )
 
-        def s_abs(i, c):
-            nc.scalar.activation(out=new("xa", i, c)[:], in_=st[("gp", i, c)][:], func=ACT.Abs, scale=c2[:, c : c + 1])
-
-        def v_sign(i, c):
-            nc.vector.tensor_scalar(
-                out=new("sg", i, c)[:], in0=st[("gp", i, c)][:], scalar1=0.0, scalar2=2.0, op0=ALU.is_ge, op1=ALU.mult
-            )
-
-        def s_sqrt(i, c):
+        def x_abs(i, c):
             nc.scalar.activation(
-                out=new("lt", i, c)[:], in_=st[("q6", i, c)][:], func=ACT.Sqrt, bias=ones2[:, 0:1], scale=6.0
+                out=unit("xa", i, c)[:], in_=live[("g", i, c)][:], func=ACT.Abs, scale=x_c[:, c : c + 1]
             )
 
-        def v6(i, c):
-            lt = st[("lt", i, c)]
-            nc.vector.tensor_tensor(out=lt[:], in0=lt[:], in1=st[("xa", i, c)][:], op=ALU.add)
+        def x_sign(i, c):
+            nc.scalar.activation(out=unit("sg", i, c)[:], in_=live[("g", i, c)][:], func=ACT.Sign)
 
-        def g7(i, c):
-            ns = new("ns", i, c)
-            nc.gpsimd.tensor_scalar(
-                out=ns[:], in0=st[("q6", i, c)][:], scalar1=1.0, scalar2=-1.0, op0=ALU.mult, op1=ALU.add
+        def root(i, c):
+            nc.scalar.activation(
+                out=unit("t", i, c)[:], in_=live[("q6", i, c)][:], func=ACT.Sqrt, bias=one[:], scale=6.0
             )
-            nc.gpsimd.tensor_tensor(out=ns[:], in0=ns[:], in1=st[("xa", i, c)][:], op=ALU.mult)
 
-        def s_ln_t(i, c):
-            lt = st[("lt", i, c)]
-            nc.scalar.activation(out=lt[:], in_=lt[:], func=ACT.Ln)
+        def t_add(i, c):
+            t = live[("t", i, c)]
+            nc.vector.tensor_tensor(out=t[:], in0=t[:], in1=live[("xa", i, c)][:], op=ALU.add)
 
-        def v8(i, c):
-            lt = st[("lt", i, c)]
+        def series(i, c):
             nc.vector.scalar_tensor_tensor(
-                out=lt[:], in0=st[("q6", i, c)][:], scalar=THR6, in1=lt[:], op0=ALU.is_ge, op1=ALU.mult
-            )
-
-        def v9(i, c):
-            lt = st[("lt", i, c)]
-            nc.vector.scalar_tensor_tensor(
-                out=lt[:], in0=lt[:], scalar=-1.0, in1=st[("ns", i, c)][:], op0=ALU.mult, op1=ALU.min
-            )
-
-        def v10(i, c):
-            nc.vector.scalar_tensor_tensor(
-                out=new("ot", i, c)[:],
-                in0=st[("sg", i, c)][:],
+                out=unit("ns", i, c)[:],
+                in0=live[("q6", i, c)][:],
                 scalar=1.0,
-                in1=st[("lt", i, c)][:],
+                in1=live[("xa", i, c)][:],
                 op0=ALU.subtract,
                 op1=ALU.mult,
             )
 
-        def v11(i, c):
-            ot = st[("ot", i, c)]
-            nc.vector.tensor_scalar(
-                out=ot[:], in0=ot[:], scalar1=w2[:, c : c + 1], scalar2=cap[:, c : c + 1], op0=ALU.mult, op1=ALU.max
+        def t_ln(i, c):
+            t = live[("t", i, c)]
+            nc.scalar.activation(out=t[:], in_=t[:], func=ACT.Ln)
+
+        def log_mask(i, c):
+            t = live[("t", i, c)]
+            nc.vector.scalar_tensor_tensor(
+                out=t[:], in0=live[("q6", i, c)][:], scalar=SMALL_Q6, in1=t[:], op0=ALU.is_ge, op1=ALU.mult
             )
-            nc.sync.dma_start(out=out[i, c * P : (c + 1) * P].rearrange("k h w -> k (h w)"), in_=ot[:])
 
-        def both(f, i):
-            f(i, 0)
-            f(i, 1)
+        def pick(i, c):
+            t = live[("t", i, c)]
+            nc.vector.scalar_tensor_tensor(
+                out=t[:], in0=t[:], scalar=-1.0, in1=live[("ns", i, c)][:], op0=ALU.mult, op1=ALU.min
+            )
 
-        def stage_y(i):
-            y_fill(i, 0)
-            y_fill(i, 1)
-            y_mult(i, 0)
-            y_mult(i, 1)
-            y_quant(i)
+        def signed(i, c):
+            nc.vector.scalar_tensor_tensor(
+                out=unit("o", i, c)[:],
+                in0=live[("t", i, c)][:],
+                scalar=w2_c[:, c : c + 1],
+                in1=live[("sg", i, c)][:],
+                op0=ALU.mult,
+                op1=ALU.mult,
+            )
 
-        sq_s(0)
-        sq_v(0)
-        nt_pe(0)
-        sq_s(1)
-        sq_v(1)
-        nt_pe(1)
-        cls_sums_s()
+        def cap_store(i, c):
+            o = live[("o", i, c)]
+            nc.vector.tensor_scalar(out=o[:], in0=o[:], scalar1=cap_c[:, c : c + 1], scalar2=None, op0=ALU.max)
+            nc.sync.dma_start(out=out[i, c * P : (c + 1) * P].rearrange("k h w -> k (h w)"), in_=o[:])
+
+        def stage_last(i):
+            for stage in (log_mask, pick, signed, cap_store):
+                both(stage, i)
+
+        for b in range(2):
+            square_s(b)
+            square_v(b)
+            norm_transpose(b, 0)
+            norm_transpose(b, 1)
+        class_sums()
         for i in range(4):
-            w_regroup(i)
-        nt_red(0)
-        sq_s(2)
-        sq_v(2)
+            w_sort(i)
+        norm_reduce(0)
+        square_s(2)
+        square_v(2)
         for i in range(3):
             w_transpose(i)
         for i in range(3):
-            w_evac(i)
+            w_group(i)
         w_transpose(3)
-        nt_pe(2, (0,))
-        sq_s(3)
-        nt_red(1)
-        nt_pe(2, (1,))
-        chain_v0(0, 16)
-        chain_sqrt(0, 16)
-        chain_tanh(0, 16)
-        sq_v(3)
-        w_evac(3)
-        chain_v1(0, 16)
-        y_fill(0, 0)
-        y_fill(0, 1)
-        nt_pe(3)
-        y_mult(0, 0)
-        nt_red(2)
-        y_mult(0, 1)
-        nt_red(3)
-        chain_v0(16, 32)
-        chain_sqrt(16, 32)
-        chain_tanh(16, 32)
-        y_quant(0)
-        w_quant()
-        cls_consts()
-        for blk in range(2):
-            uh_stage(blk)
-        mx_first(0)
-        both(g_hs, 0)
-        stage_a(0)
-        chain_v1(16, 32)
-        nc.scalar.activation(out=lnk[:], in_=bw5[:], func=ACT.Ln)
+        norm_transpose(2, 0)
+        square_s(3)
+        norm_reduce(1)
+        norm_transpose(2, 1)
+        pixel_floor(0, 2)
+        pixel_sqrt(0, 2)
+        pixel_tanh(0, 2)
+        square_v(3)
+        w_group(3)
+        pixel_values(0, 2)
+        y_spread(0)
+        norm_transpose(3, 0)
+        norm_transpose(3, 1)
+        y_scale(0, 0)
+        norm_reduce(2)
+        y_scale(0, 1)
+        norm_reduce(3)
+        pixel_floor(2, NB)
+        pixel_sqrt(2, NB)
+        pixel_tanh(2, NB)
+        y_quantise(0)
+        w_quantise()
+        class_constants()
+        spread_to_sbuf(uh_px, uh_t, 0)
+        mx_ahead(0)
+        spread_to_sbuf(rv_px, rv_t, 0)
+        stage_front(0)
+        pixel_values(2, NB)
+        nc.scalar.activation(out=lnk_c[:], in_=k_c[:], func=ACT.Ln)
         stage_y(1)
 
         for i in range(NB):
             if i > 0:
-                both(s_ln_t, i - 1)
-            if i + 1 < NB:
-                uh_stage(2 * i + 2)
-            s_ln_d(i, 0)
-            if i + 1 < NB:
-                uh_stage(2 * i + 3)
-            s_ln_d(i, 1)
-            rv_fill(i)
-            both(s_exp, i)
+                both(t_ln, i - 1)
+            both(den_ln, i)
+            both(den_exp, i)
             if i > 0:
-                for f in (v8, v9, v10, v11):
-                    both(f, i - 1)
+                stage_last(i - 1)
             if i + 1 < NB:
-                mx_first(i + 1)
-            both(v45, i)
-            both(v_sign, i)
+                spread_to_sbuf(uh_px, uh_t, i + 1)
+                mx_ahead(i + 1)
+                spread_to_sbuf(rv_px, rv_t, i + 1)
+            both(g_clamp, i)
             if i + 1 < NB:
                 for c in range(CT):
-                    s_square(i, c)
-                    s_abs(i, c)
-                    g7(i, c)
-                both(s_sqrt, i)
+                    q_scalar(i, c)
+                    x_abs(i, c)
+                    x_sign(i, c)
             else:
-                both(v_square, i)
-                both(s_abs, i)
-                both(g7, i)
-                both(s_sqrt, i)
+                both(q_vector, i)
+                both(x_abs, i)
+            both(root, i)
             if i + 1 < NB:
-                both(g_hs, i + 1)
-                stage_a(i + 1)
+                stage_front(i + 1)
             if i + 2 < NB:
-                y_fill(i + 2, 0)
-                y_fill(i + 2, 1)
-                y_mult(i + 2, 0)
-                y_mult(i + 2, 1)
-            both(v6, i)
-            if i + 2 < NB:
-                y_quant(i + 2)
-        both(s_ln_t, NB - 1)
-        for f in (v8, v9, v10, v11):
-            both(f, NB - 1)
+                stage_y(i + 2)
+            both(t_add, i)
+            both(series, i)
+        both(t_ln, NB - 1)
+        both(x_sign, NB - 1)
+        stage_last(NB - 1)

@@ -186,13 +186,16 @@ def tile_hyperboliclayer_kernel(tc, z, p, normals, out):
         def square_v(b):
             t = sqp.tile([P, 2, NPX], F32, tag="sq_v", name="sq_v")
             nc.vector.tensor_tensor(out=t[:], in0=zt[b][:, 2:4, :], in1=zt[b][:, 2:4, :], op=ALU.mult)
+            if b < 2:
+                nc.vector.tensor_tensor(out=t[:, 0, :], in0=t[:, 0, :], in1=t[:, 1, :], op=ALU.add)
             live[("sq_v", b)] = t
 
         def norm_transpose(b, h):
             nt = bank("sb" if b == 0 else "st")
             for c4 in range(4):
                 cols = slice((4 * h + c4) * P, (4 * h + c4 + 1) * P)
-                for j in range(PACK):
+                terms = PACK - 1 if b < 2 else PACK
+                for j in range(terms):
                     sq = live[("sq_s", b)] if j < 2 else live[("sq_v", b)]
                     nc.tensor.matmul(
                         out=nt[:, c4, :],
@@ -200,7 +203,7 @@ def tile_hyperboliclayer_kernel(tc, z, p, normals, out):
                         rhs=ident_f[:],
                         is_transpose=True,
                         start=(j == 0),
-                        stop=(j == PACK - 1),
+                        stop=(j == terms - 1),
                     )
             live[("nt", b, h)] = nt
 
@@ -492,7 +495,7 @@ def tile_hyperboliclayer_kernel(tc, z, p, normals, out):
                 mx_ahead(i + 1)
                 spread_to_sbuf(rv_px, rv_t, i + 1)
             both(g_clamp, i)
-            if i + 1 < NB:
+            if i + 2 < NB:
                 for c in range(CT):
                     q_scalar(i, c)
                     x_abs(i, c)
@@ -501,6 +504,8 @@ def tile_hyperboliclayer_kernel(tc, z, p, normals, out):
                 both(q_vector, i)
                 both(x_abs, i)
             both(root, i)
+            if i + 2 == NB:
+                both(x_sign, i)
             if i + 1 < NB:
                 stage_front(i + 1)
             if i + 2 < NB:

import math
from contextlib import ExitStack

import concourse.mybir as mybir
from concourse.masks import make_identity

F32 = mybir.dt.float32
BF16 = mybir.dt.bfloat16
U32 = mybir.dt.uint32
U8 = mybir.dt.uint8
FP8X4 = mybir.dt.float8_e4m3fn_x4
ALU = mybir.AluOpType
ACT = mybir.ActivationFunctionType
AX = mybir.AxisListType

P = 128
PACK = 4
D = P * PACK
NB = 4
NPX = 1024
BLK = 512
CT = 2
CHUNKS = NPX // P
FLOPS = 2 * 2 * CT * P * D * NB * NPX

ASINH_85 = math.log(85.0 + math.sqrt(85.0 * 85.0 + 1.0))
SMALL_Q6 = 0.01 * 0.01 / 6.0

PSUM_BUFS = {"aw": 3, "sb": 2, "st": 3}


def tile_hyperboliclayer_kernel(tc, z, p, normals, out):
    nc = tc.nc
    with ExitStack() as ctx:
        ctx.enter_context(tc.manual_schedule())
        keep = ctx.enter_context(tc.tile_pool(name="keep", bufs=1))
        psum = ctx.enter_context(tc.psum_pool(name="psum", bufs=2))

        ident_b = keep.tile([P, P], BF16, name="ident_b")
        make_identity(nc, ident_b[:])
        ident_f = keep.tile([P, P], F32, name="ident_f")
        make_identity(nc, ident_f[:])
        one = keep.tile([P, 1], F32, name="one")
        nc.vector.memset(one[:], 1.0)

        p_raw = keep.tile([P, CT, D], BF16, name="p_raw")
        n_raw = keep.tile([P, CT, D], BF16, name="n_raw")
        nc.scalar.dma_start(out=p_raw[:], in_=p.rearrange("(c k) d -> k c d", k=P))
        nc.scalar.dma_start(out=n_raw[:], in_=normals.rearrange("(c k) d -> k c d", k=P))
        zt = []
        for b in range(NB):
            zb = keep.tile([P, PACK, NPX], BF16, name="z%d" % b)
            nc.sync.dma_start(out=zb[:], in_=z[b].rearrange("(q j) h w -> q j (h w)", j=PACK))
            zt.append(zb)

        warm = keep.tile([P, 1], F32, name="warm")
        nc.scalar.activation(out=warm[:], in_=one[:], func=ACT.Sqrt)

        w_codes = keep.tile([P, 4 * P], U32, name="w_codes", align_bytes=64)
        w_scales = keep.tile([P, 4 * P], U8, name="w_scales", align_bytes=64)
        ppww = keep.tile([P, 2 * CT], F32, name="ppww")
        pwp = keep.tile([P, CT], F32, name="pwp")

        def per_class(name):
            return keep.tile([P, CT], F32, name=name)

        b_c = per_class("b_c")
        rb_c = per_class("rb_c")
        r_c = per_class("r_c")
        nb_c = per_class("nb_c")
        hb_c = per_class("hb_c")
        bw_c = per_class("bw_c")
        kcap_c = per_class("kcap_c")
        k_c = per_class("k_c")
        lnk_c = per_class("lnk_c")
        rw_c = per_class("rw_c")
        x_c = per_class("x_c")
        xq_c = per_class("xq_c")
        w2_c = per_class("w2_c")
        cap_c = per_class("cap_c")
        xqq_c = per_class("xqq_c")

        s_px = keep.tile([P, NB * CHUNKS], F32, name="s_px")
        uh_px = keep.tile([P, NB * CHUNKS], F32, name="uh_px")
        rv_px = keep.tile([P, NB * CHUNKS], F32, name="rv_px")
        nsq_px = keep.tile([P, NB * CHUNKS], F32, name="nsq_px")
        n_px = keep.tile([P, NB * CHUNKS], F32, name="n_px")
        th_px = keep.tile([P, NB * CHUNKS], F32, name="th_px")
        rn_px = keep.tile([P, NB * CHUNKS], F32, name="rn_px")
        zz_px = keep.tile([P, NB * CHUNKS], F32, name="zz_px")
        v_px = keep.tile([P, NB * CHUNKS], F32, name="v_px")
        uh_t = keep.tile([P, NB * NPX], F32, name="uh_t")
        rv_t = keep.tile([P, NB * NPX], F32, name="rv_t")

        wtmp = ctx.enter_context(tc.tile_pool(name="wtmp", bufs=1))
        sqp = ctx.enter_context(tc.tile_pool(name="sqp", bufs=2))
        ep = ctx.enter_context(tc.tile_pool(name="ep", bufs=2))
        live = {}

        def bank(tag):
            return psum.tile([P, 4, P], F32, tag=tag, name=tag, bufs=PSUM_BUFS[tag])

        def flat(t):
            return t[:].rearrange("q a b -> q (a b)")

        def half(h):
            return slice(h * BLK, (h + 1) * BLK)

        def unit(tag, i, c):
            t = ep.tile([P, NPX], F32, tag=tag, name=tag)
            live[(tag, i, c)] = t
            return t

        def both(stage, i):
            stage(i, 0)
            stage(i, 1)

        w_grouped = wtmp.tile([P, 4, P, PACK], BF16, name="w_grouped", align_bytes=64)
        sq_junk = wtmp.tile([P, D], F32, name="sq_junk")
        pn_t = wtmp.tile([P, CT, D], F32, name="pn_t")

        def w_sort(i):
            raw = p_raw if i < CT else n_raw
            src = raw[:, i % CT, :].rearrange("k (q t) -> k t q", t=PACK)
            srt = wtmp.tile([P, PACK, P], BF16, name="w_sorted%d" % i)
            if i < CT:
                nc.vector.tensor_scalar(out=srt[:], in0=src, scalar1=-1.0, scalar2=None, op0=ALU.mult)
            else:
                nc.vector.tensor_copy(out=srt[:], in_=src)
            live[("w_sorted", i)] = srt

        def w_transpose(i):
            tp = psum.tile([P, PACK, P], BF16, tag="aw", name="w_t%d" % i, bufs=PSUM_BUFS["aw"])
            for t in range(PACK):
                nc.tensor.transpose(out=tp[:, t, :], in_=live[("w_sorted", i)][:, t, :], identity=ident_b[:])
            live[("w_t", i)] = tp

        def w_group(i):
            nc.vector.tensor_copy(out=w_grouped[:, i, :, :], in_=live[("w_t", i)][:].rearrange("q t k -> q k t"))

        def w_quantise():
            nc.vector.quantize_mx(
                out=w_codes[:].bitcast(FP8X4), scales=w_scales[:], in_=w_grouped[:].rearrange("q i k t -> q (i k t)")
            )

        def class_sums():
            for c in range(CT):
                nc.scalar.activation(
                    out=sq_junk[:], in_=p_raw[:, c, :], func=ACT.Square, accum_out=ppww[:, c : c + 1]
                )
            for c in range(CT):
                nc.scalar.activation(
                    out=sq_junk[:], in_=n_raw[:, c, :], func=ACT.Square, accum_out=ppww[:, CT + c : CT + c + 1]
                )

        def class_constants():
            def scaled(dst, src, factor):
                nc.vector.tensor_scalar(out=dst[:], in0=src, scalar1=factor, scalar2=None, op0=ALU.mult)

            pp = ppww[:, 0:CT]
            ww = ppww[:, CT : 2 * CT]
            nc.vector.tensor_tensor(out=pn_t[:], in0=p_raw[:], in1=n_raw[:], op=ALU.mult)
            nc.vector.reduce_sum(out=pwp[:], in_=pn_t[:], axis=AX.X)
            nc.vector.tensor_scalar(out=b_c[:], in0=pp, scalar1=-1.0, scalar2=1.0, op0=ALU.mult, op1=ALU.add)
            nc.vector.reciprocal(out=rb_c[:], in_=b_c[:])
            nc.vector.scalar_tensor_tensor(
                out=r_c[:], in0=pwp[:], scalar=-2.0, in1=rb_c[:], op0=ALU.mult, op1=ALU.mult
            )
            scaled(nb_c, b_c[:], -1.0)
            scaled(hb_c, b_c[:], 0.5)
            nc.vector.tensor_tensor(out=bw_c[:], in0=b_c[:], in1=ww, op=ALU.mult)
            scaled(kcap_c, bw_c[:], 1.0e10)
            scaled(k_c, bw_c[:], 0.5e5)
            nc.vector.reciprocal(out=rw_c[:], in_=ww)
            scaled(x_c, rw_c[:], 2.0)
            scaled(xq_c, rw_c[:], 2.0 / math.sqrt(6.0))
            nc.vector.tensor_tensor(out=xqq_c[:], in0=xq_c[:], in1=xq_c[:], op=ALU.mult)
            scaled(w2_c, ww, 2.0)
            scaled(cap_c, ww, -2.0 * ASINH_85)

        def square_s(b):
            t = sqp.tile([P, 2, NPX], F32, tag="sq_s", name="sq_s")
            nc.scalar.activation(out=t[:], in_=zt[b][:, 0:2, :], func=ACT.Square)
            live[("sq_s", b)] = t

        def square_v(b):
            t = sqp.tile([P, 2, NPX], F32, tag="sq_v", name="sq_v")
            nc.vector.tensor_tensor(out=t[:], in0=zt[b][:, 2:4, :], in1=zt[b][:, 2:4, :], op=ALU.mult)
            if b < 2:
                nc.vector.tensor_tensor(out=t[:, 0, :], in0=t[:, 0, :], in1=t[:, 1, :], op=ALU.add)
            live[("sq_v", b)] = t

        def norm_transpose(b, h):
            nt = bank("sb" if b == 0 else "st")
            for c4 in range(4):
                cols = slice((4 * h + c4) * P, (4 * h + c4 + 1) * P)
                terms = PACK - 1 if b < 2 else PACK
                for j in range(terms):
                    sq = live[("sq_s", b)] if j < 2 else live[("sq_v", b)]
                    nc.tensor.matmul(
                        out=nt[:, c4, :],
                        lhsT=sq[:, j % 2, cols],
                        rhs=ident_f[:],
                        is_transpose=True,
                        start=(j == 0),
                        stop=(j == terms - 1),
                    )
            live[("nt", b, h)] = nt

        def norm_reduce(b):
            for h in range(2):
                k = CHUNKS * b + 4 * h
                nc.vector.reduce_sum(out=nsq_px[:, k : k + 4], in_=live[("nt", b, h)][:], axis=AX.X)

        def px(t, b0, b1):
            return t[:, CHUNKS * b0 : CHUNKS * b1]

        def pixel_floor(b0, b1):
            nc.vector.tensor_scalar(
                out=px(n_px, b0, b1), in0=px(nsq_px, b0, b1), scalar1=1.0e-30, scalar2=None, op0=ALU.max
            )

        def pixel_sqrt(b0, b1):
            nc.scalar.activation(out=px(n_px, b0, b1), in_=px(n_px, b0, b1), func=ACT.Sqrt)

        def pixel_tanh(b0, b1):
            nc.scalar.activation(out=px(th_px, b0, b1), in_=px(n_px, b0, b1), func=ACT.Tanh)

        def pixel_values(b0, b1):
            th = px(th_px, b0, b1)
            zz = px(zz_px, b0, b1)
            nc.vector.reciprocal(out=px(rn_px, b0, b1), in_=px(n_px, b0, b1))
            nc.vector.tensor_tensor(out=px(s_px, b0, b1), in0=th, in1=px(rn_px, b0, b1), op=ALU.mult)
            nc.vector.tensor_tensor(out=zz, in0=th, in1=th, op=ALU.mult)
            nc.vector.tensor_scalar(out=px(uh_px, b0, b1), in0=zz, scalar1=0.5, scalar2=0.5, op0=ALU.mult, op1=ALU.add)
            nc.vector.tensor_scalar(out=px(v_px, b0, b1), in0=zz, scalar1=-1.0, scalar2=1.0, op0=ALU.mult, op1=ALU.add)
            nc.vector.reciprocal(out=px(rv_px, b0, b1), in_=px(v_px, b0, b1))

        def spread(values, i, h, tag):
            t = bank(tag)
            for j in range(4):
                col = CHUNKS * i + 4 * h + j
                nc.tensor.transpose(
                    out=t[:, j, :], in_=values[:, col : col + 1].to_broadcast([P, P]), identity=ident_f[:]
                )
            return t

        def spread_to_sbuf(values, dst, i):
            for h in range(2):
                t = spread(values, i, h, "st")
                nc.scalar.copy(out=dst[:, i * NPX + h * BLK : i * NPX + (h + 1) * BLK], in_=flat(t))

        def y_spread(i):
            for h in range(2):
                live[("s", i, h)] = spread(s_px, i, h, "sb")

        def y_scale(i, h):
            if h == 0:
                live[("y", i)] = ep.tile([P, NPX, PACK], BF16, tag="y", name="y", align_bytes=64, bufs=1)
            nc.vector.tensor_tensor(
                out=live[("y", i)][:, half(h), :],
                in0=zt[i][:, :, half(h)].rearrange("q j n -> q n j"),
                in1=flat(live[("s", i, h)]).unsqueeze(2).to_broadcast([P, BLK, PACK]),
                op=ALU.mult,
            )

        def y_quantise(i):
            codes = ep.tile([P, NPX], U32, tag="y_codes", name="y_codes", align_bytes=64)
            scales = ep.tile([P, NPX], U8, tag="y_scales", name="y_scales", align_bytes=64)
            nc.vector.quantize_mx(
                out=codes[:].bitcast(FP8X4), scales=scales[:], in_=live[("y", i)][:].rearrange("q n j -> q (n j)")
            )
            live[("y_codes", i)] = codes
            live[("y_scales", i)] = scales

        def stage_y(i):
            y_spread(i)
            y_scale(i, 0)
            y_scale(i, 1)
            y_quantise(i)

        def mx(operand, i, h):
            acc = bank("aw")
            nc.tensor.matmul_mx(
                out=flat(acc),
                lhsT=w_codes[:, operand * P : (operand + 1) * P].bitcast(FP8X4),
                lhsT_scale=w_scales[:, operand * P : (operand + 1) * P],
                rhs=live[("y_codes", i)][:, half(h)].bitcast(FP8X4),
                rhs_scale=live[("y_scales", i)][:, half(h)],
                start=True,
                stop=True,
            )
            live[("mx", i, operand, h)] = acc

        def e_add(i, c, h):
            nc.vector.tensor_tensor(
                out=live[("e", i, c)][:, half(h)],
                in0=flat(live[("mx", i, c, h)]),
                in1=uh_t[:, i * NPX + h * BLK : i * NPX + (h + 1) * BLK],
                op=ALU.add,
            )

        def g_form(i, c, h):
            nc.vector.scalar_tensor_tensor(
                out=live[("g", i, c)][:, half(h)],
                in0=live[("e", i, c)][:, half(h)],
                scalar=r_c[:, c : c + 1],
                in1=flat(live[("mx", i, CT + c, h)]),
                op0=ALU.mult,
                op1=ALU.add,
            )

        def den_form(i, c):
            nc.vector.scalar_tensor_tensor(
                out=live[("k", i, c)][:],
                in0=uh_t[:, i * NPX : (i + 1) * NPX],
                scalar=nb_c[:, c : c + 1],
                in1=live[("e", i, c)][:],
                op0=ALU.mult,
                op1=ALU.add,
            )

        def mx_ahead(i):
            mx(0, i, 0)
            mx(0, i, 1)
            mx(CT, i, 0)

        def stage_front(i):
            for c in range(CT):
                unit("e", i, c)
                live[("g", i, c)] = ep.tile([P, NPX], F32, tag="g", name="g", bufs=4)
                unit("k", i, c)
                if c == 1:
                    mx(1, i, 1)
                    mx(CT + 1, i, 0)
                e_add(i, c, 0)
                mx(CT + c, i, 1)
                e_add(i, c, 1)
                if c == 0:
                    mx(1, i, 0)
                g_form(i, c, 0)
                g_form(i, c, 1)
                den_form(i, c)

        def den_ln(i, c):
            k = live[("k", i, c)]
            nc.scalar.activation(out=k[:], in_=k[:], func=ACT.Ln, bias=hb_c[:, c : c + 1], scale=1.0)

        def den_exp(i, c):
            k = live[("k", i, c)]
            nc.scalar.activation(out=k[:], in_=k[:], func=ACT.Exp, bias=lnk_c[:, c : c + 1], scale=-1.0)

        def g_clamp(i, c):
            k = live[("k", i, c)]
            g = live[("g", i, c)]
            nc.vector.scalar_tensor_tensor(
                out=k[:],
                in0=k[:],
                scalar=kcap_c[:, c : c + 1],
                in1=rv_t[:, i * NPX : (i + 1) * NPX],
                op0=ALU.min,
                op1=ALU.min,
            )
            nc.vector.tensor_tensor(out=g[:], in0=g[:], in1=k[:], op=ALU.mult)

        def q_scalar(i, c):
            nc.scalar.activation(
                out=unit("q6", i, c)[:], in_=live[("g", i, c)][:], func=ACT.Square, scale=xq_c[:, c : c + 1]
            )

        def q_vector(i, c):
            g = live[("g", i, c)]
            nc.vector.scalar_tensor_tensor(
                out=unit("q6", i, c)[:], in0=g[:], scalar=xqq_c[:, c : c + 1], in1=g[:], op0=ALU.mult, op1=ALU.mult
            )

        def x_abs(i, c):
            nc.scalar.activation(
                out=unit("xa", i, c)[:], in_=live[("g", i, c)][:], func=ACT.Abs, scale=x_c[:, c : c + 1]
            )

        def x_sign(i, c):
            nc.scalar.activation(out=unit("sg", i, c)[:], in_=live[("g", i, c)][:], func=ACT.Sign)

        def root(i, c):
            nc.scalar.activation(
                out=unit("t", i, c)[:], in_=live[("q6", i, c)][:], func=ACT.Sqrt, bias=one[:], scale=6.0
            )

        def t_add(i, c):
            t = live[("t", i, c)]
            nc.vector.tensor_tensor(out=t[:], in0=t[:], in1=live[("xa", i, c)][:], op=ALU.add)

        def series(i, c):
            nc.vector.scalar_tensor_tensor(
                out=unit("ns", i, c)[:],
                in0=live[("q6", i, c)][:],
                scalar=1.0,
                in1=live[("xa", i, c)][:],
                op0=ALU.subtract,
                op1=ALU.mult,
            )

        def t_ln(i, c):
            t = live[("t", i, c)]
            nc.scalar.activation(out=t[:], in_=t[:], func=ACT.Ln)

        def log_mask(i, c):
            t = live[("t", i, c)]
            nc.vector.scalar_tensor_tensor(
                out=t[:], in0=live[("q6", i, c)][:], scalar=SMALL_Q6, in1=t[:], op0=ALU.is_ge, op1=ALU.mult
            )

        def pick(i, c):
            t = live[("t", i, c)]
            nc.vector.scalar_tensor_tensor(
                out=t[:], in0=t[:], scalar=-1.0, in1=live[("ns", i, c)][:], op0=ALU.mult, op1=ALU.min
            )

        def signed(i, c):
            nc.vector.scalar_tensor_tensor(
                out=unit("o", i, c)[:],
                in0=live[("t", i, c)][:],
                scalar=w2_c[:, c : c + 1],
                in1=live[("sg", i, c)][:],
                op0=ALU.mult,
                op1=ALU.mult,
            )

        def cap_store(i, c):
            o = live[("o", i, c)]
            nc.vector.tensor_scalar(out=o[:], in0=o[:], scalar1=cap_c[:, c : c + 1], scalar2=None, op0=ALU.max)
            nc.sync.dma_start(out=out[i, c * P : (c + 1) * P].rearrange("k h w -> k (h w)"), in_=o[:])

        def stage_last(i):
            for stage in (log_mask, pick, signed, cap_store):
                both(stage, i)

        for b in range(2):
            square_s(b)
            square_v(b)
            norm_transpose(b, 0)
            norm_transpose(b, 1)
        class_sums()
        for i in range(4):
            w_sort(i)
        norm_reduce(0)
        square_s(2)
        square_v(2)
        for i in range(3):
            w_transpose(i)
        for i in range(3):
            w_group(i)
        w_transpose(3)
        norm_transpose(2, 0)
        square_s(3)
        norm_reduce(1)
        norm_transpose(2, 1)
        pixel_floor(0, 2)
        pixel_sqrt(0, 2)
        pixel_tanh(0, 2)
        square_v(3)
        w_group(3)
        pixel_values(0, 2)
        y_spread(0)
        norm_transpose(3, 0)
        norm_transpose(3, 1)
        y_scale(0, 0)
        norm_reduce(2)
        y_scale(0, 1)
        norm_reduce(3)
        pixel_floor(2, NB)
        pixel_sqrt(2, NB)
        pixel_tanh(2, NB)
        y_quantise(0)
        w_quantise()
        class_constants()
        spread_to_sbuf(uh_px, uh_t, 0)
        mx_ahead(0)
        spread_to_sbuf(rv_px, rv_t, 0)
        stage_front(0)
        pixel_values(2, NB)
        nc.scalar.activation(out=lnk_c[:], in_=k_c[:], func=ACT.Ln)
        stage_y(1)

        for i in range(NB):
            if i > 0:
                both(t_ln, i - 1)
            both(den_ln, i)
            both(den_exp, i)
            if i > 0:
                stage_last(i - 1)
            if i + 1 < NB:
                spread_to_sbuf(uh_px, uh_t, i + 1)
                mx_ahead(i + 1)
                spread_to_sbuf(rv_px, rv_t, i + 1)
            both(g_clamp, i)
            if i + 2 < NB:
                for c in range(CT):
                    q_scalar(i, c)
                    x_abs(i, c)
                    x_sign(i, c)
            else:
                both(q_vector, i)
                both(x_abs, i)
            both(root, i)
            if i + 2 == NB:
                both(x_sign, i)
            if i + 1 < NB:
                stage_front(i + 1)
            if i + 2 < NB:
                stage_y(i + 2)
            both(t_add, i)
            both(series, i)
        both(t_ln, NB - 1)
        both(x_sign, NB - 1)
        stage_last(NB - 1)
